import numpy as np
import ml_dtypes


def mxq(x, axis, fmt="e4m3"):
    dtype, down = {"e4m3": (ml_dtypes.float8_e4m3fn, 7), "e5m2": (ml_dtypes.float8_e5m2, 14)}[fmt]
    v = np.moveaxis(np.asarray(x, np.float32).astype(ml_dtypes.bfloat16).astype(np.float64), axis, -1)
    blocks = v.reshape(v.shape[:-1] + (-1, 32))
    amax = np.abs(blocks).max(-1, keepdims=True)
    byte = np.maximum(np.where(amax > 0, np.frexp(amax)[1] - 1 + 127, 0) - down, 1)
    scale = np.exp2(byte - 127.0)
    codes = (blocks / scale).astype(np.float32).astype(dtype).astype(np.float64)
    return np.moveaxis((codes * scale).reshape(v.shape), -1, axis)


BF16 = ml_dtypes.bfloat16


def bf(x):
    return np.asarray(x, np.float32).astype(BF16)


def f64(x):
    return np.asarray(x).astype(np.float64)


B, C, H, W, PATCH = 4, 512, 64, 64, 4
TEMPERATURE = 0.1


def _prep(x):
    x = x.reshape(B, C, H // PATCH, PATCH, W // PATCH, PATCH).mean(axis=(3, 5))
    norm = np.sqrt(np.sum(x * x, axis=1, keepdims=True))
    x = x / np.maximum(norm, 1e-12)
    return x.reshape(B, C, -1).transpose(0, 2, 1)


def log_softmax(v):
    v = v - v.max(-1, keepdims=True)
    return v - np.log(np.exp(v).sum(-1, keepdims=True))


def setup_inputs():
    g = 1.0 / PATCH
    feat_S = np.random.standard_normal((B, C, H, W)) + g * np.random.standard_normal((1, C, 1, 1))
    feat_T = np.random.standard_normal((B, C, H, W)) + g * np.random.standard_normal((1, C, 1, 1))
    return {"feat_S": bf(feat_S), "feat_T": bf(feat_T)}


def reference(feat_S, feat_T):
    qS = mxq(_prep(f64(feat_S)), 2, "e4m3")
    qT = mxq(_prep(f64(feat_T)), 2, "e4m3")
    N = qS.shape[1]
    sims_S = (qS[:, None] @ qS[None].transpose(0, 1, 3, 2)) / TEMPERATURE
    sims_T = (qT[:, None] @ qT[None].transpose(0, 1, 3, 2)) / TEMPERATURE
    log_p_s = log_softmax(sims_S)
    log_p_t = log_softmax(sims_T)
    p_t = np.exp(log_p_t)
    kl = np.sum(p_t * (log_p_t - log_p_s), axis=(-1, -2)) / N
    return np.mean(kl)

@@ -1,0 +1,258 @@
+from contextlib import ExitStack
+
+import concourse.mybir as mybir
+from concourse.masks import make_identity
+
+F32 = mybir.dt.float32
+BF16 = mybir.dt.bfloat16
+U32 = mybir.dt.uint32
+U8 = mybir.dt.uint8
+FP8X4 = mybir.dt.float8_e4m3fn_x4
+ACT = mybir.ActivationFunctionType
+ALU = mybir.AluOpType
+AX = mybir.AxisListType
+
+P = 128
+IMAGES = 4
+CHANNELS = 512
+SIDE = 64
+PATCH = 4
+GRID = SIDE // PATCH
+PIXELS = GRID * GRID
+PACK = CHANNELS // P
+STRIP = PATCH * SIDE
+STRIPS = PACK * GRID
+HALVES = PIXELS // P
+ROWS = IMAGES * PIXELS
+ROW_TILES = ROWS // P
+BANK = 512
+BANKS_PER_ROW = ROWS // BANK
+GROUPS = ROW_TILES * IMAGES
+INV_TEMPERATURE = 10.0
+NORM_FLOOR_SQUARED = (PATCH * PATCH * 1e-12) ** 2
+
+GPSIMD_STRIPS = 23
+VECTOR_STRIPS = STRIPS - GPSIMD_STRIPS
+
+FLOPS = 2 * IMAGES * IMAGES * 2 * PIXELS * PIXELS * CHANNELS
+
+
+def load_and_pool(nc, pools, image):
+    planes = image.rearrange("(p j) h w -> p j (h w)", j=PACK)
+    raw = pools["raw"].tile([P, PACK, SIDE * SIDE], BF16)
+    for j in range(PACK):
+        nc.sync.dma_start(out=raw[:, j, :], in_=planes[:, j, :])
+    strips = raw[:].rearrange("p j (y e) -> p (j y) e", e=STRIP)
+    sums = pools["sums"].tile([P, STRIPS, GRID], F32)
+
+    for first in range(0, VECTOR_STRIPS, GRID):
+        last = min(first + GRID, VECTOR_STRIPS)
+        nc.vector.tensor_reduce(
+            out=sums[:, first:last, :],
+            in_=strips[:, first:last, :].rearrange(
+                "p s (dy x dx) -> p s x dy dx", dy=PATCH, dx=PATCH
+            ),
+            axis=AX.XY,
+            op=ALU.add,
+        )
+
+    mine = strips[:, VECTOR_STRIPS:STRIPS, :]
+    two_rows = pools["tree"].tile([P, GPSIMD_STRIPS, 2 * SIDE], F32)
+    nc.gpsimd.tensor_tensor(
+        out=two_rows[:], in0=mine[:, :, 0 : 2 * SIDE], in1=mine[:, :, 2 * SIDE : 4 * SIDE], op=ALU.add
+    )
+    one_row = pools["tree"].tile([P, GPSIMD_STRIPS, SIDE], F32)
+    nc.gpsimd.tensor_tensor(
+        out=one_row[:], in0=two_rows[:, :, 0:SIDE], in1=two_rows[:, :, SIDE : 2 * SIDE], op=ALU.add
+    )
+    quads = one_row[:].rearrange("p s (x dx) -> p s x dx", dx=PATCH)
+    pairs = pools["tree"].tile([P, GPSIMD_STRIPS, GRID, 2], F32)
+    nc.gpsimd.tensor_tensor(
+        out=pairs[:], in0=quads[:, :, :, 0:2], in1=quads[:, :, :, 2:4], op=ALU.add
+    )
+    nc.gpsimd.tensor_tensor(
+        out=sums[:, VECTOR_STRIPS:STRIPS, :], in0=pairs[:, :, :, 0], in1=pairs[:, :, :, 1], op=ALU.add
+    )
+    return sums
+
+
+def normalise(nc, pools, consts, sums):
+    flat = sums[:].rearrange("p s x -> p (s x)")
+    square_sum = pools["small"].tile([P, HALVES], F32)
+    turned = []
+    for half in range(HALVES):
+        by_pixel = pools["psum_turn"].tile([P, PACK, P], F32)
+        for j in range(PACK):
+            start = j * PIXELS + half * P
+            nc.tensor.transpose(by_pixel[:, j, :], flat[:, start : start + P], consts["ident_f32"][:])
+        squares = pools["scratch"].tile([P, CHANNELS], F32)
+        nc.scalar.activation(
+            out=squares[:],
+            in_=by_pixel[:].rearrange("n j p -> n (j p)"),
+            func=ACT.Square,
+            accum_out=square_sum[:, half : half + 1],
+        )
+        turned.append(by_pixel)
+
+    floored = pools["small"].tile([P, HALVES], F32)
+    nc.vector.tensor_scalar_max(out=floored[:], in0=square_sum[:], scalar1=NORM_FLOOR_SQUARED)
+    inv_square = pools["small"].tile([P, HALVES], F32)
+    nc.vector.reciprocal(out=inv_square[:], in_=floored[:])
+    inv_norm = pools["small"].tile([P, HALVES], F32)
+    nc.scalar.activation(out=inv_norm[:], in_=inv_square[:], func=ACT.Sqrt)
+
+    unit = pools["work"].tile([P, HALVES, CHANNELS], BF16)
+    for half in range(HALVES):
+        nc.scalar.activation(
+            out=unit[:, half, :],
+            in_=turned[half][:].rearrange("n j p -> n (j p)"),
+            func=ACT.Copy,
+            scale=inv_norm[:, half : half + 1],
+        )
+    back = pools["psum_back"].tile([P, PACK, PIXELS], BF16)
+    for half in range(HALVES):
+        for j in range(PACK):
+            nc.tensor.transpose(
+                back[:, j, half * P : (half + 1) * P],
+                unit[:, half, j * P : (j + 1) * P],
+                consts["ident_bf16"][:],
+            )
+    return back
+
+
+def quantise(nc, pools, back, sign, codes, scales):
+    grouped = pools["work"].tile([P, PIXELS, PACK], BF16, align_bytes=64)
+    nc.scalar.activation(
+        out=grouped[:], in_=back[:].rearrange("p j n -> p n j"), func=ACT.Copy, scale=sign
+    )
+    nc.vector.quantize_mx(
+        out=codes.bitcast(FP8X4), scales=scales, in_=grouped[:].rearrange("p n j -> p (n j)")
+    )
+
+
+def similarity(nc, acc, left, right, row_tile, bank, start, stop):
+    rows = slice(row_tile * P, (row_tile + 1) * P)
+    cols = slice(bank * BANK, (bank + 1) * BANK)
+    nc.tensor.matmul_mx(
+        out=acc,
+        lhsT=left["codes"][:, rows].bitcast(FP8X4),
+        lhsT_scale=left["scales"][:, rows],
+        rhs=right["codes"][:, cols].bitcast(FP8X4),
+        rhs_scale=right["scales"][:, cols],
+        start=start,
+        stop=stop,
+    )
+
+
+def tile_criterionminibatchcrossimagepair_kernel(tc, feat_S, feat_T, out):
+    nc = tc.nc
+    with ExitStack() as ctx:
+        pools = {
+            "const": ctx.enter_context(tc.tile_pool(name="const", bufs=1)),
+            "raw": ctx.enter_context(tc.tile_pool(name="raw", bufs=4)),
+            "tree": ctx.enter_context(tc.tile_pool(name="tree", bufs=2)),
+            "sums": ctx.enter_context(tc.tile_pool(name="sums", bufs=2)),
+            "small": ctx.enter_context(tc.tile_pool(name="small", bufs=2)),
+            "work": ctx.enter_context(tc.tile_pool(name="work", bufs=2)),
+            "scratch": ctx.enter_context(tc.tile_pool(name="scratch", bufs=4)),
+            "psum_turn": ctx.enter_context(tc.psum_pool(name="psum_turn", bufs=2)),
+            "psum_back": ctx.enter_context(tc.psum_pool(name="psum_back", bufs=1)),
+            "psum_sim": ctx.enter_context(tc.psum_pool(name="psum_sim", bufs=3)),
+            "psum_dif": ctx.enter_context(tc.psum_pool(name="psum_dif", bufs=2)),
+        }
+        const = pools["const"]
+        ident_f32 = const.tile([P, P], F32)
+        make_identity(nc, ident_f32[:])
+        ident_bf16 = const.tile([P, P], BF16)
+        make_identity(nc, ident_bf16[:])
+        ones = const.tile([P, P], F32)
+        nc.vector.memset(ones[:], 1.0)
+        consts = {"ident_f32": ident_f32, "ident_bf16": ident_bf16}
+
+        operands = {}
+        for name in ("S", "minus_S", "T"):
+            codes = const.tile([P, ROWS], U32, name="codes_" + name, align_bytes=64)
+            scales = const.tile([P, ROWS], U8, name="scales_" + name, align_bytes=64)
+            operands[name] = {"codes": codes, "scales": scales}
+        z_s = const.tile([P, GROUPS], F32)
+        z_t = const.tile([P, GROUPS], F32)
+        cross = const.tile([P, GROUPS], F32)
+
+        for feat, names in ((feat_S, (("S", 1.0), ("minus_S", -1.0))), (feat_T, (("T", 1.0),))):
+            for b in range(IMAGES):
+                sums = load_and_pool(nc, pools, feat[b])
+                back = normalise(nc, pools, consts, sums)
+                cols = slice(b * PIXELS, (b + 1) * PIXELS)
+                for name, sign in names:
+                    quantise(
+                        nc, pools, back, sign,
+                        operands[name]["codes"][:, cols], operands[name]["scales"][:, cols],
+                    )
+            if feat is feat_S:
+                for row_tile in range(ROW_TILES):
+                    for bank in range(BANKS_PER_ROW):
+                        sim = pools["psum_sim"].tile([P, BANK], F32, tag="sim")
+                        similarity(nc, sim[:], operands["S"], operands["S"], row_tile, bank, True, True)
+                        for k in range(BANK // PIXELS):
+                            group = row_tile * IMAGES + bank * (BANK // PIXELS) + k
+                            exp_s = pools["scratch"].tile([P, PIXELS], F32)
+                            nc.scalar.activation(
+                                out=exp_s[:],
+                                in_=sim[:, k * PIXELS : (k + 1) * PIXELS],
+                                func=ACT.Exp,
+                                scale=INV_TEMPERATURE,
+                                bias=-INV_TEMPERATURE,
+                                accum_out=z_s[:, group : group + 1],
+                            )
+
+        for row_tile in range(ROW_TILES):
+            for bank in range(BANKS_PER_ROW):
+                sim = pools["psum_sim"].tile([P, BANK], F32, tag="sim")
+                similarity(nc, sim[:], operands["T"], operands["T"], row_tile, bank, True, True)
+                dif = pools["psum_dif"].tile([P, BANK], F32)
+                similarity(nc, dif[:], operands["T"], operands["T"], row_tile, bank, True, False)
+                similarity(nc, dif[:], operands["S"], operands["minus_S"], row_tile, bank, False, True)
+                exp_t = pools["work"].tile([P, BANK], F32)
+                for k in range(BANK // PIXELS):
+                    group = row_tile * IMAGES + bank * (BANK // PIXELS) + k
+                    part = slice(k * PIXELS, (k + 1) * PIXELS)
+                    nc.scalar.activation(
+                        out=exp_t[:, part],
+                        in_=sim[:, part],
+                        func=ACT.Exp,
+                        scale=INV_TEMPERATURE,
+                        bias=-INV_TEMPERATURE,
+                        accum_out=z_t[:, group : group + 1],
+                    )
+                    product = pools["scratch"].tile([P, PIXELS], F32)
+                    nc.vector.scalar_tensor_tensor(
+                        out=product[:],
+                        in0=dif[:, part],
+                        scalar=INV_TEMPERATURE,
+                        in1=exp_t[:, part],
+                        op0=ALU.mult,
+                        op1=ALU.mult,
+                        accum_out=cross[:, group : group + 1],
+                    )
+
+        inv_z = pools["small"].tile([P, GROUPS], F32)
+        nc.vector.reciprocal(out=inv_z[:], in_=z_t[:])
+        expected = pools["small"].tile([P, GROUPS], F32)
+        nc.vector.tensor_mul(out=expected[:], in0=cross[:], in1=inv_z[:])
+        ratio = pools["small"].tile([P, GROUPS], F32)
+        nc.vector.tensor_mul(out=ratio[:], in0=z_s[:], in1=inv_z[:])
+        log_ratio = pools["small"].tile([P, GROUPS], F32)
+        nc.scalar.activation(out=log_ratio[:], in_=ratio[:], func=ACT.Ln)
+        total = pools["psum_sim"].tile([P, GROUPS], F32, tag="sim")
+        nc.tensor.matmul(out=total[:], lhsT=ones[:], rhs=expected[:], start=True, stop=False)
+        nc.tensor.matmul(out=total[:], lhsT=ones[:], rhs=log_ratio[:], start=False, stop=True)
+        scaled = pools["small"].tile([P, GROUPS], F32)
+        mean = pools["small"].tile([P, 1], F32)
+        nc.scalar.activation(
+            out=scaled[:], in_=total[:], func=ACT.Copy,
+            scale=1.0 / (IMAGES * IMAGES * PIXELS), accum_out=mean[:],
+        )
+        out_view = out
+        for extra in range(2 - len(out.shape)):
+            out_view = out_view.unsqueeze(0)
+        nc.sync.dma_start(out=out_view, in_=mean[0:1, 0:1])

@@ -20,236 +20,255 @@ PATCH = 4
 GRID = SIDE // PATCH
 PIXELS = GRID * GRID
 PACK = CHANNELS // P
-STRIP = PATCH * SIDE
-STRIPS = PACK * GRID
 HALVES = PIXELS // P
 ROWS = IMAGES * PIXELS
 ROW_TILES = ROWS // P
 BANK = 512
-BANKS_PER_ROW = ROWS // BANK
 GROUPS = ROW_TILES * IMAGES
 INV_TEMPERATURE = 10.0
 NORM_FLOOR_SQUARED = (PATCH * PATCH * 1e-12) ** 2
 
-GPSIMD_STRIPS = 23
-VECTOR_STRIPS = STRIPS - GPSIMD_STRIPS
+STACKS = 2
+ALL_IMAGES = STACKS * IMAGES
+ROW_PAIRS = PATCH // 2
+STEPS = PACK * ROW_PAIRS
+PLACES = ROW_PAIRS * PATCH
+LOADS_AHEAD = 3
+
+SQUARE_STEP = 0
+NORMALISE_STEP = 3
+TURN_BACK_STEP = 4
+QUANTISE_STEP = 7
 
 FLOPS = 2 * IMAGES * IMAGES * 2 * PIXELS * PIXELS * CHANNELS
 
 
-def load_and_pool(nc, pools, image):
-    planes = image.rearrange("(p j) h w -> p j (h w)", j=PACK)
-    raw = pools["raw"].tile([P, PACK, SIDE * SIDE], BF16)
-    for j in range(PACK):
-        nc.sync.dma_start(out=raw[:, j, :], in_=planes[:, j, :])
-    strips = raw[:].rearrange("p j (y e) -> p (j y) e", e=STRIP)
-    sums = pools["sums"].tile([P, STRIPS, GRID], F32)
-
-    for first in range(0, VECTOR_STRIPS, GRID):
-        last = min(first + GRID, VECTOR_STRIPS)
-        nc.vector.tensor_reduce(
-            out=sums[:, first:last, :],
-            in_=strips[:, first:last, :].rearrange(
-                "p s (dy x dx) -> p s x dy dx", dy=PATCH, dx=PATCH
-            ),
-            axis=AX.XY,
-            op=ALU.add,
-        )
-
-    mine = strips[:, VECTOR_STRIPS:STRIPS, :]
-    two_rows = pools["tree"].tile([P, GPSIMD_STRIPS, 2 * SIDE], F32)
-    nc.gpsimd.tensor_tensor(
-        out=two_rows[:], in0=mine[:, :, 0 : 2 * SIDE], in1=mine[:, :, 2 * SIDE : 4 * SIDE], op=ALU.add
-    )
-    one_row = pools["tree"].tile([P, GPSIMD_STRIPS, SIDE], F32)
-    nc.gpsimd.tensor_tensor(
-        out=one_row[:], in0=two_rows[:, :, 0:SIDE], in1=two_rows[:, :, SIDE : 2 * SIDE], op=ALU.add
-    )
-    quads = one_row[:].rearrange("p s (x dx) -> p s x dx", dx=PATCH)
-    pairs = pools["tree"].tile([P, GPSIMD_STRIPS, GRID, 2], F32)
-    nc.gpsimd.tensor_tensor(
-        out=pairs[:], in0=quads[:, :, :, 0:2], in1=quads[:, :, :, 2:4], op=ALU.add
-    )
-    nc.gpsimd.tensor_tensor(
-        out=sums[:, VECTOR_STRIPS:STRIPS, :], in0=pairs[:, :, :, 0], in1=pairs[:, :, :, 1], op=ALU.add
-    )
-    return sums
-
-
-def normalise(nc, pools, consts, sums):
-    flat = sums[:].rearrange("p s x -> p (s x)")
-    square_sum = pools["small"].tile([P, HALVES], F32)
-    turned = []
-    for half in range(HALVES):
-        by_pixel = pools["psum_turn"].tile([P, PACK, P], F32)
-        for j in range(PACK):
-            start = j * PIXELS + half * P
-            nc.tensor.transpose(by_pixel[:, j, :], flat[:, start : start + P], consts["ident_f32"][:])
-        squares = pools["scratch"].tile([P, CHANNELS], F32)
-        nc.scalar.activation(
-            out=squares[:],
-            in_=by_pixel[:].rearrange("n j p -> n (j p)"),
-            func=ACT.Square,
-            accum_out=square_sum[:, half : half + 1],
-        )
-        turned.append(by_pixel)
-
-    floored = pools["small"].tile([P, HALVES], F32)
-    nc.vector.tensor_scalar_max(out=floored[:], in0=square_sum[:], scalar1=NORM_FLOOR_SQUARED)
-    inv_square = pools["small"].tile([P, HALVES], F32)
-    nc.vector.reciprocal(out=inv_square[:], in_=floored[:])
-    inv_norm = pools["small"].tile([P, HALVES], F32)
-    nc.scalar.activation(out=inv_norm[:], in_=inv_square[:], func=ACT.Sqrt)
-
-    unit = pools["work"].tile([P, HALVES, CHANNELS], BF16)
-    for half in range(HALVES):
-        nc.scalar.activation(
-            out=unit[:, half, :],
-            in_=turned[half][:].rearrange("n j p -> n (j p)"),
-            func=ACT.Copy,
-            scale=inv_norm[:, half : half + 1],
-        )
-    back = pools["psum_back"].tile([P, PACK, PIXELS], BF16)
-    for half in range(HALVES):
-        for j in range(PACK):
-            nc.tensor.transpose(
-                back[:, j, half * P : (half + 1) * P],
-                unit[:, half, j * P : (j + 1) * P],
-                consts["ident_bf16"][:],
-            )
-    return back
-
-
-def quantise(nc, pools, back, sign, codes, scales):
-    grouped = pools["work"].tile([P, PIXELS, PACK], BF16, align_bytes=64)
-    nc.scalar.activation(
-        out=grouped[:], in_=back[:].rearrange("p j n -> p n j"), func=ACT.Copy, scale=sign
-    )
-    nc.vector.quantize_mx(
-        out=codes.bitcast(FP8X4), scales=scales, in_=grouped[:].rearrange("p n j -> p (n j)")
-    )
-
-
-def similarity(nc, acc, left, right, row_tile, bank, start, stop):
-    rows = slice(row_tile * P, (row_tile + 1) * P)
-    cols = slice(bank * BANK, (bank + 1) * BANK)
-    nc.tensor.matmul_mx(
-        out=acc,
-        lhsT=left["codes"][:, rows].bitcast(FP8X4),
-        lhsT_scale=left["scales"][:, rows],
-        rhs=right["codes"][:, cols].bitcast(FP8X4),
-        rhs_scale=right["scales"][:, cols],
-        start=start,
-        stop=stop,
-    )
+def new_pairs(b):
+    return [(b, j) for j in range(b + 1)] + [(i, b) for i in range(b)]
 
 
 def tile_criterionminibatchcrossimagepair_kernel(tc, feat_S, feat_T, out):
     nc = tc.nc
     with ExitStack() as ctx:
-        pools = {
-            "const": ctx.enter_context(tc.tile_pool(name="const", bufs=1)),
-            "raw": ctx.enter_context(tc.tile_pool(name="raw", bufs=4)),
-            "tree": ctx.enter_context(tc.tile_pool(name="tree", bufs=2)),
-            "sums": ctx.enter_context(tc.tile_pool(name="sums", bufs=2)),
-            "small": ctx.enter_context(tc.tile_pool(name="small", bufs=2)),
-            "work": ctx.enter_context(tc.tile_pool(name="work", bufs=2)),
-            "scratch": ctx.enter_context(tc.tile_pool(name="scratch", bufs=4)),
-            "psum_turn": ctx.enter_context(tc.psum_pool(name="psum_turn", bufs=2)),
-            "psum_back": ctx.enter_context(tc.psum_pool(name="psum_back", bufs=1)),
-            "psum_sim": ctx.enter_context(tc.psum_pool(name="psum_sim", bufs=3)),
-            "psum_dif": ctx.enter_context(tc.psum_pool(name="psum_dif", bufs=2)),
-        }
-        const = pools["const"]
+        const = ctx.enter_context(tc.tile_pool(name="const", bufs=1))
+        raw_pool = ctx.enter_context(tc.tile_pool(name="raw", bufs=LOADS_AHEAD + 1))
+        partial_pool = ctx.enter_context(tc.tile_pool(name="partial", bufs=6))
+        small = ctx.enter_context(tc.tile_pool(name="small", bufs=2))
+        work = ctx.enter_context(tc.tile_pool(name="work", bufs=2))
+        scratch = ctx.enter_context(tc.tile_pool(name="scratch", bufs=4))
+        psum_turn = ctx.enter_context(tc.psum_pool(name="psum_turn", bufs=2 * HALVES))
+        psum_back = ctx.enter_context(tc.psum_pool(name="psum_back", bufs=1))
+        psum_pair = ctx.enter_context(tc.psum_pool(name="psum_pair", bufs=3))
+
         ident_f32 = const.tile([P, P], F32)
         make_identity(nc, ident_f32[:])
         ident_bf16 = const.tile([P, P], BF16)
         make_identity(nc, ident_bf16[:])
         ones = const.tile([P, P], F32)
         nc.vector.memset(ones[:], 1.0)
-        consts = {"ident_f32": ident_f32, "ident_bf16": ident_bf16}
 
         operands = {}
         for name in ("S", "minus_S", "T"):
             codes = const.tile([P, ROWS], U32, name="codes_" + name, align_bytes=64)
             scales = const.tile([P, ROWS], U8, name="scales_" + name, align_bytes=64)
             operands[name] = {"codes": codes, "scales": scales}
-        z_s = const.tile([P, GROUPS], F32)
-        z_t = const.tile([P, GROUPS], F32)
-        cross = const.tile([P, GROUPS], F32)
+        z_s = const.tile([P, IMAGES, HALVES, IMAGES], F32)
+        z_t = const.tile([P, IMAGES, HALVES, IMAGES], F32)
+        cross = const.tile([P, IMAGES, HALVES, IMAGES], F32)
 
-        for feat, names in ((feat_S, (("S", 1.0), ("minus_S", -1.0))), (feat_T, (("T", 1.0),))):
-            for b in range(IMAGES):
-                sums = load_and_pool(nc, pools, feat[b])
-                back = normalise(nc, pools, consts, sums)
-                cols = slice(b * PIXELS, (b + 1) * PIXELS)
-                for name, sign in names:
-                    quantise(
-                        nc, pools, back, sign,
-                        operands[name]["codes"][:, cols], operands[name]["scales"][:, cols],
-                    )
-            if feat is feat_S:
-                for row_tile in range(ROW_TILES):
-                    for bank in range(BANKS_PER_ROW):
-                        sim = pools["psum_sim"].tile([P, BANK], F32, tag="sim")
-                        similarity(nc, sim[:], operands["S"], operands["S"], row_tile, bank, True, True)
-                        for k in range(BANK // PIXELS):
-                            group = row_tile * IMAGES + bank * (BANK // PIXELS) + k
-                            exp_s = pools["scratch"].tile([P, PIXELS], F32)
-                            nc.scalar.activation(
-                                out=exp_s[:],
-                                in_=sim[:, k * PIXELS : (k + 1) * PIXELS],
-                                func=ACT.Exp,
-                                scale=INV_TEMPERATURE,
-                                bias=-INV_TEMPERATURE,
-                                accum_out=z_s[:, group : group + 1],
-                            )
+        raw = {}
+        by_pixel = {}
+        square_sum = {}
+        back = {}
+        grouped = {}
+        dif = {}
+        exp_t = {}
 
-        for row_tile in range(ROW_TILES):
-            for bank in range(BANKS_PER_ROW):
-                sim = pools["psum_sim"].tile([P, BANK], F32, tag="sim")
-                similarity(nc, sim[:], operands["T"], operands["T"], row_tile, bank, True, True)
-                dif = pools["psum_dif"].tile([P, BANK], F32)
-                similarity(nc, dif[:], operands["T"], operands["T"], row_tile, bank, True, False)
-                similarity(nc, dif[:], operands["S"], operands["minus_S"], row_tile, bank, False, True)
-                exp_t = pools["work"].tile([P, BANK], F32)
-                for k in range(BANK // PIXELS):
-                    group = row_tile * IMAGES + bank * (BANK // PIXELS) + k
-                    part = slice(k * PIXELS, (k + 1) * PIXELS)
-                    nc.scalar.activation(
-                        out=exp_t[:, part],
-                        in_=sim[:, part],
-                        func=ACT.Exp,
-                        scale=INV_TEMPERATURE,
-                        bias=-INV_TEMPERATURE,
-                        accum_out=z_t[:, group : group + 1],
-                    )
-                    product = pools["scratch"].tile([P, PIXELS], F32)
-                    nc.vector.scalar_tensor_tensor(
-                        out=product[:],
-                        in0=dif[:, part],
-                        scalar=INV_TEMPERATURE,
-                        in1=exp_t[:, part],
-                        op0=ALU.mult,
-                        op1=ALU.mult,
-                        accum_out=cross[:, group : group + 1],
+        def is_teacher(k):
+            return k >= IMAGES
+
+        def load(k):
+            feat = feat_T if is_teacher(k) else feat_S
+            planes = feat[k % IMAGES].rearrange("(p j) h w -> p j (h w)", j=PACK)
+            raw[k] = raw_pool.tile([P, PACK, SIDE * SIDE], BF16, name="raw")
+            for j in range(PACK):
+                nc.sync.dma_start(out=raw[k][:, j, :], in_=planes[:, j, :])
+
+        def add_rows(k, step):
+            j, dy = divmod(step, ROW_PAIRS)
+            if step == 0:
+                by_pixel[k] = [
+                    psum_turn.tile([P, PACK, P], F32, name="by_pixel") for half in range(HALVES)
+                ]
+            spread = raw[k][:, j, :].rearrange(
+                "p (y dy x dx) -> p dy dx y x", dy=PATCH, x=GRID, dx=PATCH
+            )
+            partial = partial_pool.tile([P, PATCH, PIXELS], F32)
+            nc.vector.tensor_tensor(
+                out=partial[:].rearrange("p dx (y x) -> p dx y x", x=GRID),
+                in0=spread[:, dy],
+                in1=spread[:, dy + ROW_PAIRS],
+                op=ALU.add,
+            )
+            for half in range(HALVES):
+                for dx in range(PATCH):
+                    nc.tensor.matmul(
+                        out=by_pixel[k][half][:, j, :],
+                        lhsT=partial[:, dx, half * P : (half + 1) * P],
+                        rhs=ident_f32[:],
+                        is_transpose=True,
+                        start=(dy == 0 and dx == 0),
+                        stop=(dy == ROW_PAIRS - 1 and dx == PATCH - 1),
                     )
 
-        inv_z = pools["small"].tile([P, GROUPS], F32)
-        nc.vector.reciprocal(out=inv_z[:], in_=z_t[:])
-        expected = pools["small"].tile([P, GROUPS], F32)
-        nc.vector.tensor_mul(out=expected[:], in0=cross[:], in1=inv_z[:])
-        ratio = pools["small"].tile([P, GROUPS], F32)
-        nc.vector.tensor_mul(out=ratio[:], in0=z_s[:], in1=inv_z[:])
-        log_ratio = pools["small"].tile([P, GROUPS], F32)
+        def square_sums(k):
+            square_sum[k] = small.tile([P, HALVES], F32, name="square_sum")
+            for half in range(HALVES):
+                squares = scratch.tile([P, CHANNELS], F32)
+                nc.scalar.activation(
+                    out=squares[:],
+                    in_=by_pixel[k][half][:].rearrange("n j p -> n (j p)"),
+                    func=ACT.Square,
+                    accum_out=square_sum[k][:, half : half + 1],
+                )
+
+        def normalise(k):
+            floored = small.tile([P, HALVES], F32)
+            nc.vector.tensor_scalar_max(out=floored[:], in0=square_sum[k][:], scalar1=NORM_FLOOR_SQUARED)
+            inv_square = small.tile([P, HALVES], F32)
+            nc.vector.reciprocal(out=inv_square[:], in_=floored[:])
+            inv_norm = small.tile([P, HALVES], F32)
+            nc.scalar.activation(out=inv_norm[:], in_=inv_square[:], func=ACT.Sqrt)
+            unit = work.tile([P, HALVES, CHANNELS], BF16)
+            for half in range(HALVES):
+                nc.scalar.activation(
+                    out=unit[:, half, :],
+                    in_=by_pixel[k][half][:].rearrange("n j p -> n (j p)"),
+                    func=ACT.Copy,
+                    scale=inv_norm[:, half : half + 1],
+                )
+            return unit
+
+        def turn_back(k, unit):
+            back[k] = psum_back.tile([P, PACK, PIXELS], BF16, name="back")
+            for half in range(HALVES):
+                for j in range(PACK):
+                    nc.tensor.transpose(
+                        back[k][:, j, half * P : (half + 1) * P],
+                        unit[:, half, j * P : (j + 1) * P],
+                        ident_bf16[:],
+                    )
+            signs = (("T", 1.0),) if is_teacher(k) else (("S", 1.0), ("minus_S", -1.0))
+            grouped[k] = []
+            for name, sign in signs:
+                words = work.tile([P, PIXELS, PACK], BF16, name="grouped", align_bytes=64)
+                nc.scalar.activation(
+                    out=words[:], in_=back[k][:].rearrange("p j n -> p n j"), func=ACT.Copy, scale=sign
+                )
+                grouped[k].append((name, words))
+
+        def quantise(k):
+            cols = slice((k % IMAGES) * PIXELS, (k % IMAGES + 1) * PIXELS)
+            for name, words in grouped[k]:
+                nc.vector.quantize_mx(
+                    out=operands[name]["codes"][:, cols].bitcast(FP8X4),
+                    scales=operands[name]["scales"][:, cols],
+                    in_=words[:].rearrange("p n j -> p (n j)"),
+                )
+
+        def similarity(acc, passes, i, j):
+            cols = slice(j * PIXELS, (j + 1) * PIXELS)
+            for half in range(HALVES):
+                rows = slice(i * PIXELS + half * P, i * PIXELS + (half + 1) * P)
+                for number, (left, right) in enumerate(passes):
+                    nc.tensor.matmul_mx(
+                        out=acc[:, half, :],
+                        lhsT=operands[left]["codes"][:, rows].bitcast(FP8X4),
+                        lhsT_scale=operands[left]["scales"][:, rows],
+                        rhs=operands[right]["codes"][:, cols].bitcast(FP8X4),
+                        rhs_scale=operands[right]["scales"][:, cols],
+                        start=(number == 0),
+                        stop=(number == len(passes) - 1),
+                    )
+
+        def shifted_exp(result, sim, denominator):
+            nc.scalar.activation(
+                out=result, in_=sim, func=ACT.Exp, scale=INV_TEMPERATURE, bias=-INV_TEMPERATURE,
+                accum_out=denominator,
+            )
+
+        def start_pair(k, i, j):
+            sim = psum_pair.tile([P, HALVES, PIXELS], F32, tag="bank")
+            if is_teacher(k):
+                similarity(sim, (("T", "T"),), i, j)
+                dif[k, i, j] = psum_pair.tile([P, HALVES, PIXELS], F32, tag="bank", name="dif")
+                similarity(dif[k, i, j], (("T", "T"), ("S", "minus_S")), i, j)
+                exp_t[k, i, j] = work.tile([P, HALVES, PIXELS], F32, name="exp_t")
+                for half in range(HALVES):
+                    shifted_exp(exp_t[k, i, j][:, half, :], sim[:, half, :], z_t[:, i, half, j : j + 1])
+            else:
+                similarity(sim, (("S", "S"),), i, j)
+                for half in range(HALVES):
+                    exp_s = scratch.tile([P, PIXELS], F32)
+                    shifted_exp(exp_s[:], sim[:, half, :], z_s[:, i, half, j : j + 1])
+
+        def finish_pair(k, i, j):
+            for half in range(HALVES):
+                product = scratch.tile([P, PIXELS], F32)
+                nc.vector.scalar_tensor_tensor(
+                    out=product[:],
+                    in0=dif[k, i, j][:, half, :],
+                    scalar=INV_TEMPERATURE,
+                    in1=exp_t[k, i, j][:, half, :],
+                    op0=ALU.mult,
+                    op1=ALU.mult,
+                    accum_out=cross[:, i, half, j : j + 1],
+                )
+
+        ctx.enter_context(tc.manual_schedule())
+        for k in range(LOADS_AHEAD):
+            load(k)
+        units = {}
+        for k in range(ALL_IMAGES + 2):
+            pooled, finished, paired = k, k - 1, k - 2
+            pairs = new_pairs(paired % IMAGES) if paired >= 0 else []
+            for step in range(STEPS):
+                if step == 0 and pooled + LOADS_AHEAD < ALL_IMAGES:
+                    load(pooled + LOADS_AHEAD)
+                if pooled < ALL_IMAGES:
+                    add_rows(pooled, step)
+                if 0 <= finished < ALL_IMAGES:
+                    if step == SQUARE_STEP:
+                        square_sums(finished)
+                    if step == NORMALISE_STEP:
+                        units[finished] = normalise(finished)
+                    if step == TURN_BACK_STEP:
+                        turn_back(finished, units[finished])
+                    if step == QUANTISE_STEP:
+                        quantise(finished)
+                if step < len(pairs):
+                    start_pair(paired, pairs[step][0], pairs[step][1])
+                if 1 <= step <= len(pairs) and is_teacher(paired):
+                    finish_pair(paired, pairs[step - 1][0], pairs[step - 1][1])
+
+        def flat(t):
+            return t[:].rearrange("p i h j -> p (i h j)")
+
+        inv_z = small.tile([P, GROUPS], F32)
+        nc.vector.reciprocal(out=inv_z[:], in_=flat(z_t))
+        expected = small.tile([P, GROUPS], F32)
+        nc.vector.tensor_mul(out=expected[:], in0=flat(cross), in1=inv_z[:])
+        ratio = small.tile([P, GROUPS], F32)
+        nc.vector.tensor_mul(out=ratio[:], in0=flat(z_s), in1=inv_z[:])
+        log_ratio = small.tile([P, GROUPS], F32)
         nc.scalar.activation(out=log_ratio[:], in_=ratio[:], func=ACT.Ln)
-        total = pools["psum_sim"].tile([P, GROUPS], F32, tag="sim")
-        nc.tensor.matmul(out=total[:], lhsT=ones[:], rhs=expected[:], start=True, stop=False)
-        nc.tensor.matmul(out=total[:], lhsT=ones[:], rhs=log_ratio[:], start=False, stop=True)
-        scaled = pools["small"].tile([P, GROUPS], F32)
-        mean = pools["small"].tile([P, 1], F32)
+        total = psum_pair.tile([P, BANK], F32, tag="bank")
+        nc.tensor.matmul(out=total[:, 0:GROUPS], lhsT=ones[:], rhs=expected[:], start=True, stop=False)
+        nc.tensor.matmul(out=total[:, 0:GROUPS], lhsT=ones[:], rhs=log_ratio[:], start=False, stop=True)
+        scaled = small.tile([P, GROUPS], F32)
+        mean = small.tile([P, 1], F32)
         nc.scalar.activation(
-            out=scaled[:], in_=total[:], func=ACT.Copy,
+            out=scaled[:], in_=total[:, 0:GROUPS], func=ACT.Copy,
             scale=1.0 / (IMAGES * IMAGES * PIXELS), accum_out=mean[:],
         )
         out_view = out

@@ -35,10 +35,14 @@ STEPS = PACK * ROW_PAIRS
 PLACES = ROW_PAIRS * PATCH
 LOADS_AHEAD = 3
 
-SQUARE_STEP = 0
-NORMALISE_STEP = 3
-TURN_BACK_STEP = 4
-QUANTISE_STEP = 7
+SQUARE_DELAY = STEPS + 0
+NORMALISE_DELAY = STEPS + 3
+TURN_BACK_DELAY = STEPS + 5
+QUANTISE_DELAY = STEPS + 11
+PAIR_DELAY = STEPS + 12
+COUNTED_PERIOD = 4
+PRODUCT_LAG = 1
+LAST_STEP = STEPS * (ALL_IMAGES - 1) + PAIR_DELAY + STEPS + PRODUCT_LAG
 
 FLOPS = 2 * IMAGES * IMAGES * 2 * PIXELS * PIXELS * CHANNELS
 
@@ -112,11 +116,12 @@ def tile_criterionminibatchcrossimagepair_kernel(tc, feat_S, feat_T, out):
             )
             for half in range(HALVES):
                 for dx in range(PATCH):
+                    counted = half == 0 and dx == 1 and step % COUNTED_PERIOD != COUNTED_PERIOD - 1
                     nc.tensor.matmul(
                         out=by_pixel[k][half][:, j, :],
                         lhsT=partial[:, dx, half * P : (half + 1) * P],
                         rhs=ident_f32[:],
-                        is_transpose=True,
+                        is_transpose=not counted,
                         start=(dy == 0 and dx == 0),
                         stop=(dy == ROW_PAIRS - 1 and dx == PATCH - 1),
                     )
@@ -226,30 +231,37 @@ def tile_criterionminibatchcrossimagepair_kernel(tc, feat_S, feat_T, out):
                 )
 
         ctx.enter_context(tc.manual_schedule())
+        def due(step, delay):
+            k, since = divmod(step - delay, STEPS)
+            return (k, since) if 0 <= k < ALL_IMAGES else (None, None)
+
         for k in range(LOADS_AHEAD):
             load(k)
         units = {}
-        for k in range(ALL_IMAGES + 2):
-            pooled, finished, paired = k, k - 1, k - 2
-            pairs = new_pairs(paired % IMAGES) if paired >= 0 else []
-            for step in range(STEPS):
-                if step == 0 and pooled + LOADS_AHEAD < ALL_IMAGES:
-                    load(pooled + LOADS_AHEAD)
-                if pooled < ALL_IMAGES:
-                    add_rows(pooled, step)
-                if 0 <= finished < ALL_IMAGES:
-                    if step == SQUARE_STEP:
-                        square_sums(finished)
-                    if step == NORMALISE_STEP:
-                        units[finished] = normalise(finished)
-                    if step == TURN_BACK_STEP:
-                        turn_back(finished, units[finished])
-                    if step == QUANTISE_STEP:
-                        quantise(finished)
-                if step < len(pairs):
-                    start_pair(paired, pairs[step][0], pairs[step][1])
-                if 1 <= step <= len(pairs) and is_teacher(paired):
-                    finish_pair(paired, pairs[step - 1][0], pairs[step - 1][1])
+        for step in range(LAST_STEP + 1):
+            k, since = due(step, 0)
+            if k is not None:
+                if since == 0 and k + LOADS_AHEAD < ALL_IMAGES:
+                    load(k + LOADS_AHEAD)
+                add_rows(k, since)
+            k, since = due(step, SQUARE_DELAY)
+            if since == 0:
+                square_sums(k)
+            k, since = due(step, NORMALISE_DELAY)
+            if since == 0:
+                units[k] = normalise(k)
+            k, since = due(step, TURN_BACK_DELAY)
+            if since == 0:
+                turn_back(k, units[k])
+            k, since = due(step, QUANTISE_DELAY)
+            if since == 0:
+                quantise(k)
+            k, since = due(step, PAIR_DELAY)
+            if k is not None and since < len(new_pairs(k % IMAGES)):
+                start_pair(k, new_pairs(k % IMAGES)[since][0], new_pairs(k % IMAGES)[since][1])
+            k, since = due(step, PAIR_DELAY + PRODUCT_LAG)
+            if k is not None and is_teacher(k) and since < len(new_pairs(k % IMAGES)):
+                finish_pair(k, new_pairs(k % IMAGES)[since][0], new_pairs(k % IMAGES)[since][1])
 
         def flat(t):
             return t[:].rearrange("p i h j -> p (i h j)")

@@ -10,10 +10,10 @@ U8 = mybir.dt.uint8
 FP8X4 = mybir.dt.float8_e4m3fn_x4
 ACT = mybir.ActivationFunctionType
 ALU = mybir.AluOpType
-AX = mybir.AxisListType
 
 P = 128
 IMAGES = 4
+ALL_IMAGES = 2 * IMAGES
 CHANNELS = 512
 SIDE = 64
 PATCH = 4
@@ -22,27 +22,21 @@ PIXELS = GRID * GRID
 PACK = CHANNELS // P
 HALVES = PIXELS // P
 ROWS = IMAGES * PIXELS
-ROW_TILES = ROWS // P
-BANK = 512
-GROUPS = ROW_TILES * IMAGES
+SOFTMAXES = IMAGES * HALVES * IMAGES
 INV_TEMPERATURE = 10.0
 NORM_FLOOR_SQUARED = (PATCH * PATCH * 1e-12) ** 2
 
-STACKS = 2
-ALL_IMAGES = STACKS * IMAGES
 ROW_PAIRS = PATCH // 2
 STEPS = PACK * ROW_PAIRS
-PLACES = ROW_PAIRS * PATCH
 LOADS_AHEAD = 3
 
-SQUARE_DELAY = STEPS + 0
+SQUARE_DELAY = STEPS
 NORMALISE_DELAY = STEPS + 3
 TURN_BACK_DELAY = STEPS + 5
 QUANTISE_DELAY = STEPS + 11
 PAIR_DELAY = STEPS + 12
-COUNTED_PERIOD = 4
-PRODUCT_LAG = 1
-LAST_STEP = STEPS * (ALL_IMAGES - 1) + PAIR_DELAY + STEPS + PRODUCT_LAG
+PRODUCT_LAG = 2
+LAST_STEP = STEPS * (ALL_IMAGES - 1) + PAIR_DELAY + PRODUCT_LAG + 2 * IMAGES - 2
 
 FLOPS = 2 * IMAGES * IMAGES * 2 * PIXELS * PIXELS * CHANNELS
 
@@ -51,16 +45,21 @@ def new_pairs(b):
     return [(b, j) for j in range(b + 1)] + [(i, b) for i in range(b)]
 
 
+def due(step, delay):
+    k, count = divmod(step - delay, STEPS)
+    return (k, count) if 0 <= k < ALL_IMAGES else (None, None)
+
+
 def tile_criterionminibatchcrossimagepair_kernel(tc, feat_S, feat_T, out):
     nc = tc.nc
     with ExitStack() as ctx:
         const = ctx.enter_context(tc.tile_pool(name="const", bufs=1))
         raw_pool = ctx.enter_context(tc.tile_pool(name="raw", bufs=LOADS_AHEAD + 1))
-        partial_pool = ctx.enter_context(tc.tile_pool(name="partial", bufs=6))
+        partial_pool = ctx.enter_context(tc.tile_pool(name="partial", bufs=10))
         small = ctx.enter_context(tc.tile_pool(name="small", bufs=2))
-        work = ctx.enter_context(tc.tile_pool(name="work", bufs=2))
-        scratch = ctx.enter_context(tc.tile_pool(name="scratch", bufs=4))
-        psum_turn = ctx.enter_context(tc.psum_pool(name="psum_turn", bufs=2 * HALVES))
+        work = ctx.enter_context(tc.tile_pool(name="work", bufs=PRODUCT_LAG + 1))
+        unread = ctx.enter_context(tc.tile_pool(name="unread", bufs=4))
+        psum_sums = ctx.enter_context(tc.psum_pool(name="psum_sums", bufs=2 * HALVES))
         psum_back = ctx.enter_context(tc.psum_pool(name="psum_back", bufs=1))
         psum_pair = ctx.enter_context(tc.psum_pool(name="psum_pair", bufs=3))
 
@@ -83,7 +82,7 @@ def tile_criterionminibatchcrossimagepair_kernel(tc, feat_S, feat_T, out):
         raw = {}
         by_pixel = {}
         square_sum = {}
-        back = {}
+        unit = {}
         grouped = {}
         dif = {}
         exp_t = {}
@@ -98,30 +97,29 @@ def tile_criterionminibatchcrossimagepair_kernel(tc, feat_S, feat_T, out):
             for j in range(PACK):
                 nc.sync.dma_start(out=raw[k][:, j, :], in_=planes[:, j, :])
 
-        def add_rows(k, step):
-            j, dy = divmod(step, ROW_PAIRS)
-            if step == 0:
+        def add_rows(k, count):
+            j, dy = divmod(count, ROW_PAIRS)
+            if count == 0:
                 by_pixel[k] = [
-                    psum_turn.tile([P, PACK, P], F32, name="by_pixel") for half in range(HALVES)
+                    psum_sums.tile([P, PACK, P], F32, name="by_pixel") for half in range(HALVES)
                 ]
-            spread = raw[k][:, j, :].rearrange(
+            places = raw[k][:, j, :].rearrange(
                 "p (y dy x dx) -> p dy dx y x", dy=PATCH, x=GRID, dx=PATCH
             )
             partial = partial_pool.tile([P, PATCH, PIXELS], F32)
             nc.vector.tensor_tensor(
                 out=partial[:].rearrange("p dx (y x) -> p dx y x", x=GRID),
-                in0=spread[:, dy],
-                in1=spread[:, dy + ROW_PAIRS],
+                in0=places[:, dy],
+                in1=places[:, dy + ROW_PAIRS],
                 op=ALU.add,
             )
             for half in range(HALVES):
                 for dx in range(PATCH):
-                    counted = half == 0 and dx == 1 and step % COUNTED_PERIOD != COUNTED_PERIOD - 1
                     nc.tensor.matmul(
                         out=by_pixel[k][half][:, j, :],
                         lhsT=partial[:, dx, half * P : (half + 1) * P],
                         rhs=ident_f32[:],
-                        is_transpose=not counted,
+                        is_transpose=True,
                         start=(dy == 0 and dx == 0),
                         stop=(dy == ROW_PAIRS - 1 and dx == PATCH - 1),
                     )
@@ -129,7 +127,7 @@ def tile_criterionminibatchcrossimagepair_kernel(tc, feat_S, feat_T, out):
         def square_sums(k):
             square_sum[k] = small.tile([P, HALVES], F32, name="square_sum")
             for half in range(HALVES):
-                squares = scratch.tile([P, CHANNELS], F32)
+                squares = unread.tile([P, CHANNELS], F32)
                 nc.scalar.activation(
                     out=squares[:],
                     in_=by_pixel[k][half][:].rearrange("n j p -> n (j p)"),
@@ -144,41 +142,39 @@ def tile_criterionminibatchcrossimagepair_kernel(tc, feat_S, feat_T, out):
             nc.vector.reciprocal(out=inv_square[:], in_=floored[:])
             inv_norm = small.tile([P, HALVES], F32)
             nc.scalar.activation(out=inv_norm[:], in_=inv_square[:], func=ACT.Sqrt)
-            unit = work.tile([P, HALVES, CHANNELS], BF16)
+            unit[k] = work.tile([P, HALVES, CHANNELS], BF16, name="unit")
             for half in range(HALVES):
                 nc.scalar.activation(
-                    out=unit[:, half, :],
+                    out=unit[k][:, half, :],
                     in_=by_pixel[k][half][:].rearrange("n j p -> n (j p)"),
                     func=ACT.Copy,
                     scale=inv_norm[:, half : half + 1],
                 )
-            return unit
 
-        def turn_back(k, unit):
-            back[k] = psum_back.tile([P, PACK, PIXELS], BF16, name="back")
+        def turn_back(k):
+            back = psum_back.tile([P, PACK, PIXELS], BF16)
             for half in range(HALVES):
                 for j in range(PACK):
                     nc.tensor.transpose(
-                        back[k][:, j, half * P : (half + 1) * P],
-                        unit[:, half, j * P : (j + 1) * P],
+                        back[:, j, half * P : (half + 1) * P],
+                        unit[k][:, half, j * P : (j + 1) * P],
                         ident_bf16[:],
                     )
-            signs = (("T", 1.0),) if is_teacher(k) else (("S", 1.0), ("minus_S", -1.0))
-            grouped[k] = []
-            for name, sign in signs:
-                words = work.tile([P, PIXELS, PACK], BF16, name="grouped", align_bytes=64)
-                nc.scalar.activation(
-                    out=words[:], in_=back[k][:].rearrange("p j n -> p n j"), func=ACT.Copy, scale=sign
-                )
-                grouped[k].append((name, words))
+            grouped[k] = work.tile([P, PIXELS, PACK], BF16, name="grouped", align_bytes=64)
+            nc.scalar.copy(out=grouped[k][:], in_=back[:].rearrange("p j n -> p n j"))
 
         def quantise(k):
+            sources = [("T" if is_teacher(k) else "S", grouped[k])]
+            if not is_teacher(k):
+                negated = work.tile([P, PIXELS, PACK], BF16, align_bytes=64)
+                nc.vector.tensor_scalar_mul(out=negated[:], in0=grouped[k][:], scalar1=-1.0)
+                sources.append(("minus_S", negated))
             cols = slice((k % IMAGES) * PIXELS, (k % IMAGES + 1) * PIXELS)
-            for name, words in grouped[k]:
+            for name, values in sources:
                 nc.vector.quantize_mx(
                     out=operands[name]["codes"][:, cols].bitcast(FP8X4),
                     scales=operands[name]["scales"][:, cols],
-                    in_=words[:].rearrange("p n j -> p (n j)"),
+                    in_=values[:].rearrange("p n j -> p (n j)"),
                 )
 
         def similarity(acc, passes, i, j):
@@ -196,17 +192,17 @@ def tile_criterionminibatchcrossimagepair_kernel(tc, feat_S, feat_T, out):
                         stop=(number == len(passes) - 1),
                     )
 
-        def shifted_exp(result, sim, denominator):
+        def shifted_exp(result, sim, row_sum):
             nc.scalar.activation(
                 out=result, in_=sim, func=ACT.Exp, scale=INV_TEMPERATURE, bias=-INV_TEMPERATURE,
-                accum_out=denominator,
+                accum_out=row_sum,
             )
 
         def start_pair(k, i, j):
-            sim = psum_pair.tile([P, HALVES, PIXELS], F32, tag="bank")
+            sim = psum_pair.tile([P, HALVES, PIXELS], F32, tag="pair")
             if is_teacher(k):
                 similarity(sim, (("T", "T"),), i, j)
-                dif[k, i, j] = psum_pair.tile([P, HALVES, PIXELS], F32, tag="bank", name="dif")
+                dif[k, i, j] = psum_pair.tile([P, HALVES, PIXELS], F32, tag="pair", name="dif")
                 similarity(dif[k, i, j], (("T", "T"), ("S", "minus_S")), i, j)
                 exp_t[k, i, j] = work.tile([P, HALVES, PIXELS], F32, name="exp_t")
                 for half in range(HALVES):
@@ -214,12 +210,12 @@ def tile_criterionminibatchcrossimagepair_kernel(tc, feat_S, feat_T, out):
             else:
                 similarity(sim, (("S", "S"),), i, j)
                 for half in range(HALVES):
-                    exp_s = scratch.tile([P, PIXELS], F32)
+                    exp_s = unread.tile([P, PIXELS], F32)
                     shifted_exp(exp_s[:], sim[:, half, :], z_s[:, i, half, j : j + 1])
 
         def finish_pair(k, i, j):
             for half in range(HALVES):
-                product = scratch.tile([P, PIXELS], F32)
+                product = unread.tile([P, PIXELS], F32)
                 nc.vector.scalar_tensor_tensor(
                     out=product[:],
                     in0=dif[k, i, j][:, half, :],
@@ -231,59 +227,52 @@ def tile_criterionminibatchcrossimagepair_kernel(tc, feat_S, feat_T, out):
                 )
 
         ctx.enter_context(tc.manual_schedule())
-        def due(step, delay):
-            k, since = divmod(step - delay, STEPS)
-            return (k, since) if 0 <= k < ALL_IMAGES else (None, None)
-
+        pairs = [new_pairs(k % IMAGES) for k in range(ALL_IMAGES)]
         for k in range(LOADS_AHEAD):
             load(k)
-        units = {}
         for step in range(LAST_STEP + 1):
-            k, since = due(step, 0)
+            k, count = due(step, 0)
             if k is not None:
-                if since == 0 and k + LOADS_AHEAD < ALL_IMAGES:
+                if count == 0 and k + LOADS_AHEAD < ALL_IMAGES:
                     load(k + LOADS_AHEAD)
-                add_rows(k, since)
-            k, since = due(step, SQUARE_DELAY)
-            if since == 0:
-                square_sums(k)
-            k, since = due(step, NORMALISE_DELAY)
-            if since == 0:
-                units[k] = normalise(k)
-            k, since = due(step, TURN_BACK_DELAY)
-            if since == 0:
-                turn_back(k, units[k])
-            k, since = due(step, QUANTISE_DELAY)
-            if since == 0:
-                quantise(k)
-            k, since = due(step, PAIR_DELAY)
-            if k is not None and since < len(new_pairs(k % IMAGES)):
-                start_pair(k, new_pairs(k % IMAGES)[since][0], new_pairs(k % IMAGES)[since][1])
-            k, since = due(step, PAIR_DELAY + PRODUCT_LAG)
-            if k is not None and is_teacher(k) and since < len(new_pairs(k % IMAGES)):
-                finish_pair(k, new_pairs(k % IMAGES)[since][0], new_pairs(k % IMAGES)[since][1])
+                add_rows(k, count)
+            for stage, delay in (
+                (square_sums, SQUARE_DELAY),
+                (normalise, NORMALISE_DELAY),
+                (turn_back, TURN_BACK_DELAY),
+                (quantise, QUANTISE_DELAY),
+            ):
+                k, count = due(step, delay)
+                if count == 0:
+                    stage(k)
+            k, count = due(step, PAIR_DELAY)
+            if k is not None and count < len(pairs[k]):
+                start_pair(k, *pairs[k][count])
+            k, count = due(step, PAIR_DELAY + PRODUCT_LAG)
+            if k is not None and is_teacher(k) and count < len(pairs[k]):
+                finish_pair(k, *pairs[k][count])
 
-        def flat(t):
+        def columns(t):
             return t[:].rearrange("p i h j -> p (i h j)")
 
-        inv_z = small.tile([P, GROUPS], F32)
-        nc.vector.reciprocal(out=inv_z[:], in_=flat(z_t))
-        expected = small.tile([P, GROUPS], F32)
-        nc.vector.tensor_mul(out=expected[:], in0=flat(cross), in1=inv_z[:])
-        ratio = small.tile([P, GROUPS], F32)
-        nc.vector.tensor_mul(out=ratio[:], in0=flat(z_s), in1=inv_z[:])
-        log_ratio = small.tile([P, GROUPS], F32)
+        inv_z = small.tile([P, SOFTMAXES], F32)
+        nc.vector.reciprocal(out=inv_z[:], in_=columns(z_t))
+        expected = small.tile([P, SOFTMAXES], F32)
+        nc.vector.tensor_mul(out=expected[:], in0=columns(cross), in1=inv_z[:])
+        ratio = small.tile([P, SOFTMAXES], F32)
+        nc.vector.tensor_mul(out=ratio[:], in0=columns(z_s), in1=inv_z[:])
+        log_ratio = small.tile([P, SOFTMAXES], F32)
         nc.scalar.activation(out=log_ratio[:], in_=ratio[:], func=ACT.Ln)
-        total = psum_pair.tile([P, BANK], F32, tag="bank")
-        nc.tensor.matmul(out=total[:, 0:GROUPS], lhsT=ones[:], rhs=expected[:], start=True, stop=False)
-        nc.tensor.matmul(out=total[:, 0:GROUPS], lhsT=ones[:], rhs=log_ratio[:], start=False, stop=True)
-        scaled = small.tile([P, GROUPS], F32)
+        total = psum_pair.tile([P, HALVES, PIXELS], F32, tag="pair")
+        sums = total[:, 0, 0:SOFTMAXES]
+        nc.tensor.matmul(out=sums, lhsT=ones[:], rhs=expected[:], start=True, stop=False)
+        nc.tensor.matmul(out=sums, lhsT=ones[:], rhs=log_ratio[:], start=False, stop=True)
+        scaled = small.tile([P, SOFTMAXES], F32)
         mean = small.tile([P, 1], F32)
         nc.scalar.activation(
-            out=scaled[:], in_=total[:, 0:GROUPS], func=ACT.Copy,
-            scale=1.0 / (IMAGES * IMAGES * PIXELS), accum_out=mean[:],
+            out=scaled[:], in_=sums, func=ACT.Copy, scale=1.0 / (IMAGES * IMAGES * PIXELS), accum_out=mean[:]
         )
         out_view = out
-        for extra in range(2 - len(out.shape)):
+        for axis in range(2 - len(out.shape)):
             out_view = out_view.unsqueeze(0)
         nc.sync.dma_start(out=out_view, in_=mean[0:1, 0:1])

@@ -28,15 +28,15 @@ NORM_FLOOR_SQUARED = (PATCH * PATCH * 1e-12) ** 2
 
 ROW_PAIRS = PATCH // 2
 STEPS = PACK * ROW_PAIRS
-LOADS_AHEAD = 3
+LOADS_AHEAD = 2
 
 SQUARE_DELAY = STEPS
 NORMALISE_DELAY = STEPS + 3
 TURN_BACK_DELAY = STEPS + 5
 QUANTISE_DELAY = STEPS + 11
-PAIR_DELAY = STEPS + 12
-PRODUCT_LAG = 2
-LAST_STEP = STEPS * (ALL_IMAGES - 1) + PAIR_DELAY + PRODUCT_LAG + 2 * IMAGES - 2
+RUN_DELAY = STEPS * (IMAGES - 1) + QUANTISE_DELAY + 1 - (IMAGES - 1) ** 2
+PRODUCT_LAG = 1
+LAST_STEP = STEPS * IMAGES + RUN_DELAY + IMAGES * IMAGES - 1 + PRODUCT_LAG
 
 FLOPS = 2 * IMAGES * IMAGES * 2 * PIXELS * PIXELS * CHANNELS
 
@@ -55,9 +55,9 @@ def tile_criterionminibatchcrossimagepair_kernel(tc, feat_S, feat_T, out):
     with ExitStack() as ctx:
         const = ctx.enter_context(tc.tile_pool(name="const", bufs=1))
         raw_pool = ctx.enter_context(tc.tile_pool(name="raw", bufs=LOADS_AHEAD + 1))
-        partial_pool = ctx.enter_context(tc.tile_pool(name="partial", bufs=10))
+        partial_pool = ctx.enter_context(tc.tile_pool(name="partial", bufs=STEPS))
         small = ctx.enter_context(tc.tile_pool(name="small", bufs=2))
-        work = ctx.enter_context(tc.tile_pool(name="work", bufs=PRODUCT_LAG + 1))
+        work = ctx.enter_context(tc.tile_pool(name="work", bufs=2))
         unread = ctx.enter_context(tc.tile_pool(name="unread", bufs=4))
         psum_sums = ctx.enter_context(tc.psum_pool(name="psum_sums", bufs=2 * HALVES))
         psum_back = ctx.enter_context(tc.psum_pool(name="psum_back", bufs=1))
@@ -71,7 +71,7 @@ def tile_criterionminibatchcrossimagepair_kernel(tc, feat_S, feat_T, out):
         nc.vector.memset(ones[:], 1.0)
 
         operands = {}
-        for name in ("S", "minus_S", "T"):
+        for name in ("T", "minus_T", "S"):
             codes = const.tile([P, ROWS], U32, name="codes_" + name, align_bytes=64)
             scales = const.tile([P, ROWS], U8, name="scales_" + name, align_bytes=64)
             operands[name] = {"codes": codes, "scales": scales}
@@ -79,16 +79,17 @@ def tile_criterionminibatchcrossimagepair_kernel(tc, feat_S, feat_T, out):
         z_t = const.tile([P, IMAGES, HALVES, IMAGES], F32)
         cross = const.tile([P, IMAGES, HALVES, IMAGES], F32)
 
+        exp_t = const.tile([P, IMAGES * IMAGES, HALVES, PIXELS], F32)
+
         raw = {}
         by_pixel = {}
         square_sum = {}
         unit = {}
         grouped = {}
         dif = {}
-        exp_t = {}
 
         def is_teacher(k):
-            return k >= IMAGES
+            return k < IMAGES
 
         def load(k):
             feat = feat_T if is_teacher(k) else feat_S
@@ -165,10 +166,10 @@ def tile_criterionminibatchcrossimagepair_kernel(tc, feat_S, feat_T, out):
 
         def quantise(k):
             sources = [("T" if is_teacher(k) else "S", grouped[k])]
-            if not is_teacher(k):
+            if is_teacher(k):
                 negated = work.tile([P, PIXELS, PACK], BF16, align_bytes=64)
                 nc.vector.tensor_scalar_mul(out=negated[:], in0=grouped[k][:], scalar1=-1.0)
-                sources.append(("minus_S", negated))
+                sources.append(("minus_T", negated))
             cols = slice((k % IMAGES) * PIXELS, (k % IMAGES + 1) * PIXELS)
             for name, values in sources:
                 nc.vector.quantize_mx(
@@ -198,36 +199,36 @@ def tile_criterionminibatchcrossimagepair_kernel(tc, feat_S, feat_T, out):
                 accum_out=row_sum,
             )
 
-        def start_pair(k, i, j):
+        def teacher_pair(number, i, j):
             sim = psum_pair.tile([P, HALVES, PIXELS], F32, tag="pair")
-            if is_teacher(k):
-                similarity(sim, (("T", "T"),), i, j)
-                dif[k, i, j] = psum_pair.tile([P, HALVES, PIXELS], F32, tag="pair", name="dif")
-                similarity(dif[k, i, j], (("T", "T"), ("S", "minus_S")), i, j)
-                exp_t[k, i, j] = work.tile([P, HALVES, PIXELS], F32, name="exp_t")
-                for half in range(HALVES):
-                    shifted_exp(exp_t[k, i, j][:, half, :], sim[:, half, :], z_t[:, i, half, j : j + 1])
-            else:
-                similarity(sim, (("S", "S"),), i, j)
-                for half in range(HALVES):
-                    exp_s = unread.tile([P, PIXELS], F32)
-                    shifted_exp(exp_s[:], sim[:, half, :], z_s[:, i, half, j : j + 1])
-
-        def finish_pair(k, i, j):
+            similarity(sim, (("T", "T"),), i, j)
             for half in range(HALVES):
-                product = unread.tile([P, PIXELS], F32)
+                shifted_exp(exp_t[:, number, half, :], sim[:, half, :], z_t[:, i, half, j : j + 1])
+
+        def student_pair(number, i, j):
+            dif[number] = psum_pair.tile([P, HALVES, PIXELS], F32, tag="pair", name="dif")
+            similarity(dif[number], (("S", "S"), ("T", "minus_T")), i, j)
+            sim = psum_pair.tile([P, HALVES, PIXELS], F32, tag="pair")
+            similarity(sim, (("S", "S"),), i, j)
+            for half in range(HALVES):
+                exp_s = unread.tile([P, PIXELS], F32)
+                shifted_exp(exp_s[:], sim[:, half, :], z_s[:, i, half, j : j + 1])
+
+        def product(number, i, j):
+            for half in range(HALVES):
+                weighted = unread.tile([P, PIXELS], F32)
                 nc.vector.scalar_tensor_tensor(
-                    out=product[:],
-                    in0=dif[k, i, j][:, half, :],
-                    scalar=INV_TEMPERATURE,
-                    in1=exp_t[k, i, j][:, half, :],
+                    out=weighted[:],
+                    in0=dif[number][:, half, :],
+                    scalar=-INV_TEMPERATURE,
+                    in1=exp_t[:, number, half, :],
                     op0=ALU.mult,
                     op1=ALU.mult,
                     accum_out=cross[:, i, half, j : j + 1],
                 )
 
         ctx.enter_context(tc.manual_schedule())
-        pairs = [new_pairs(k % IMAGES) for k in range(ALL_IMAGES)]
+        pairs = [pair for b in range(IMAGES) for pair in new_pairs(b)]
         for k in range(LOADS_AHEAD):
             load(k)
         for step in range(LAST_STEP + 1):
@@ -245,12 +246,15 @@ def tile_criterionminibatchcrossimagepair_kernel(tc, feat_S, feat_T, out):
                 k, count = due(step, delay)
                 if count == 0:
                     stage(k)
-            k, count = due(step, PAIR_DELAY)
-            if k is not None and count < len(pairs[k]):
-                start_pair(k, *pairs[k][count])
-            k, count = due(step, PAIR_DELAY + PRODUCT_LAG)
-            if k is not None and is_teacher(k) and count < len(pairs[k]):
-                finish_pair(k, *pairs[k][count])
+            number = step - RUN_DELAY
+            if 0 <= number < len(pairs):
+                teacher_pair(number, *pairs[number])
+            number = step - RUN_DELAY - STEPS * IMAGES
+            if 0 <= number < len(pairs):
+                student_pair(number, *pairs[number])
+            number = number - PRODUCT_LAG
+            if 0 <= number < len(pairs):
+                product(number, *pairs[number])
 
         def columns(t):
             return t[:].rearrange("p i h j -> p (i h j)")

@@ -28,12 +28,12 @@ NORM_FLOOR_SQUARED = (PATCH * PATCH * 1e-12) ** 2
 
 ROW_PAIRS = PATCH // 2
 STEPS = PACK * ROW_PAIRS
+POOLING_STEPS = STEPS * ALL_IMAGES
 LOADS_AHEAD = 2
 
-SQUARE_DELAY = STEPS
-NORMALISE_DELAY = STEPS + 3
-TURN_BACK_DELAY = STEPS + 5
-QUANTISE_DELAY = STEPS + 11
+NORMALISE_DELAY = STEPS
+TURN_BACK_DELAY = STEPS + 3
+QUANTISE_DELAY = STEPS + 8
 RUN_DELAY = STEPS * (IMAGES - 1) + QUANTISE_DELAY + 1 - (IMAGES - 1) ** 2
 PRODUCT_LAG = 1
 LAST_STEP = STEPS * IMAGES + RUN_DELAY + IMAGES * IMAGES - 1 + PRODUCT_LAG
@@ -43,6 +43,11 @@ FLOPS = 2 * IMAGES * IMAGES * 2 * PIXELS * PIXELS * CHANNELS
 
 def new_pairs(b):
     return [(b, j) for j in range(b + 1)] + [(i, b) for i in range(b)]
+
+
+def quantise_step(k):
+    soonest = STEPS * k + QUANTISE_DELAY
+    return soonest if k < IMAGES else max(soonest, POOLING_STEPS + k % IMAGES)
 
 
 def due(step, delay):
@@ -58,6 +63,7 @@ def tile_criterionminibatchcrossimagepair_kernel(tc, feat_S, feat_T, out):
         partial_pool = ctx.enter_context(tc.tile_pool(name="partial", bufs=STEPS))
         small = ctx.enter_context(tc.tile_pool(name="small", bufs=2))
         work = ctx.enter_context(tc.tile_pool(name="work", bufs=2))
+        kept = ctx.enter_context(tc.tile_pool(name="kept", bufs=ALL_IMAGES))
         unread = ctx.enter_context(tc.tile_pool(name="unread", bufs=4))
         psum_sums = ctx.enter_context(tc.psum_pool(name="psum_sums", bufs=2 * HALVES))
         psum_back = ctx.enter_context(tc.psum_pool(name="psum_back", bufs=1))
@@ -78,18 +84,21 @@ def tile_criterionminibatchcrossimagepair_kernel(tc, feat_S, feat_T, out):
         z_s = const.tile([P, IMAGES, HALVES, IMAGES], F32)
         z_t = const.tile([P, IMAGES, HALVES, IMAGES], F32)
         cross = const.tile([P, IMAGES, HALVES, IMAGES], F32)
+        inv_z = const.tile([P, SOFTMAXES], F32)
 
         exp_t = const.tile([P, IMAGES * IMAGES, HALVES, PIXELS], F32)
 
         raw = {}
         by_pixel = {}
-        square_sum = {}
         unit = {}
         grouped = {}
         dif = {}
 
         def is_teacher(k):
             return k < IMAGES
+
+        def columns(per_softmax):
+            return per_softmax[:].rearrange("p i h j -> p (i h j)")
 
         def load(k):
             feat = feat_T if is_teacher(k) else feat_S
@@ -125,24 +134,22 @@ def tile_criterionminibatchcrossimagepair_kernel(tc, feat_S, feat_T, out):
                         stop=(dy == ROW_PAIRS - 1 and dx == PATCH - 1),
                     )
 
-        def square_sums(k):
-            square_sum[k] = small.tile([P, HALVES], F32, name="square_sum")
+        def normalise(k):
+            square_sum = small.tile([P, HALVES], F32)
             for half in range(HALVES):
                 squares = unread.tile([P, CHANNELS], F32)
                 nc.scalar.activation(
                     out=squares[:],
                     in_=by_pixel[k][half][:].rearrange("n j p -> n (j p)"),
                     func=ACT.Square,
-                    accum_out=square_sum[k][:, half : half + 1],
+                    accum_out=square_sum[:, half : half + 1],
                 )
-
-        def normalise(k):
-            floored = small.tile([P, HALVES], F32)
-            nc.vector.tensor_scalar_max(out=floored[:], in0=square_sum[k][:], scalar1=NORM_FLOOR_SQUARED)
-            inv_square = small.tile([P, HALVES], F32)
-            nc.vector.reciprocal(out=inv_square[:], in_=floored[:])
+            above_floor = small.tile([P, HALVES], F32)
+            nc.scalar.activation(out=above_floor[:], in_=square_sum[:], func=ACT.Relu, bias=-NORM_FLOOR_SQUARED)
             inv_norm = small.tile([P, HALVES], F32)
-            nc.scalar.activation(out=inv_norm[:], in_=inv_square[:], func=ACT.Sqrt)
+            nc.scalar.activation(
+                out=inv_norm[:], in_=above_floor[:], func=ACT.Abs_reciprocal_sqrt, bias=NORM_FLOOR_SQUARED
+            )
             unit[k] = work.tile([P, HALVES, CHANNELS], BF16, name="unit")
             for half in range(HALVES):
                 nc.scalar.activation(
@@ -161,22 +168,24 @@ def tile_criterionminibatchcrossimagepair_kernel(tc, feat_S, feat_T, out):
                         unit[k][:, half, j * P : (j + 1) * P],
                         ident_bf16[:],
                     )
-            grouped[k] = work.tile([P, PIXELS, PACK], BF16, name="grouped", align_bytes=64)
+            grouped[k] = kept.tile([P, PIXELS, PACK], BF16, name="grouped", align_bytes=64)
             nc.scalar.copy(out=grouped[k][:], in_=back[:].rearrange("p j n -> p n j"))
 
+        def quantise_as(name, b, values):
+            cols = slice(b * PIXELS, (b + 1) * PIXELS)
+            nc.vector.quantize_mx(
+                out=operands[name]["codes"][:, cols].bitcast(FP8X4),
+                scales=operands[name]["scales"][:, cols],
+                in_=values[:].rearrange("p n j -> p (n j)"),
+            )
+
         def quantise(k):
-            sources = [("T" if is_teacher(k) else "S", grouped[k])]
-            if is_teacher(k):
-                negated = work.tile([P, PIXELS, PACK], BF16, align_bytes=64)
-                nc.vector.tensor_scalar_mul(out=negated[:], in0=grouped[k][:], scalar1=-1.0)
-                sources.append(("minus_T", negated))
-            cols = slice((k % IMAGES) * PIXELS, (k % IMAGES + 1) * PIXELS)
-            for name, values in sources:
-                nc.vector.quantize_mx(
-                    out=operands[name]["codes"][:, cols].bitcast(FP8X4),
-                    scales=operands[name]["scales"][:, cols],
-                    in_=values[:].rearrange("p n j -> p (n j)"),
-                )
+            quantise_as("T" if is_teacher(k) else "S", k % IMAGES, grouped[k])
+
+        def quantise_negated(k):
+            negated = work.tile([P, PIXELS, PACK], BF16, align_bytes=64)
+            nc.vector.tensor_scalar_mul(out=negated[:], in0=grouped[k][:], scalar1=-1.0)
+            quantise_as("minus_T", k, negated)
 
         def similarity(acc, passes, i, j):
             cols = slice(j * PIXELS, (j + 1) * PIXELS)
@@ -237,15 +246,18 @@ def tile_criterionminibatchcrossimagepair_kernel(tc, feat_S, feat_T, out):
                 if count == 0 and k + LOADS_AHEAD < ALL_IMAGES:
                     load(k + LOADS_AHEAD)
                 add_rows(k, count)
-            for stage, delay in (
-                (square_sums, SQUARE_DELAY),
-                (normalise, NORMALISE_DELAY),
-                (turn_back, TURN_BACK_DELAY),
-                (quantise, QUANTISE_DELAY),
-            ):
+            for stage, delay in ((normalise, NORMALISE_DELAY), (turn_back, TURN_BACK_DELAY)):
                 k, count = due(step, delay)
                 if count == 0:
                     stage(k)
+            for k in range(ALL_IMAGES):
+                if step == quantise_step(k):
+                    quantise(k)
+            k = step - POOLING_STEPS
+            if 0 <= k < IMAGES:
+                quantise_negated(k)
+            if k == IMAGES:
+                nc.vector.reciprocal(out=inv_z[:], in_=columns(z_t))
             number = step - RUN_DELAY
             if 0 <= number < len(pairs):
                 teacher_pair(number, *pairs[number])
@@ -256,21 +268,17 @@ def tile_criterionminibatchcrossimagepair_kernel(tc, feat_S, feat_T, out):
             if 0 <= number < len(pairs):
                 product(number, *pairs[number])
 
-        def columns(t):
-            return t[:].rearrange("p i h j -> p (i h j)")
-
-        inv_z = small.tile([P, SOFTMAXES], F32)
-        nc.vector.reciprocal(out=inv_z[:], in_=columns(z_t))
         expected = small.tile([P, SOFTMAXES], F32)
         nc.vector.tensor_mul(out=expected[:], in0=columns(cross), in1=inv_z[:])
-        ratio = small.tile([P, SOFTMAXES], F32)
-        nc.vector.tensor_mul(out=ratio[:], in0=columns(z_s), in1=inv_z[:])
-        log_ratio = small.tile([P, SOFTMAXES], F32)
-        nc.scalar.activation(out=log_ratio[:], in_=ratio[:], func=ACT.Ln)
+        minus_log_z_t = small.tile([P, SOFTMAXES], F32)
+        nc.scalar.activation(out=minus_log_z_t[:], in_=inv_z[:], func=ACT.Ln)
+        log_z_s = small.tile([P, SOFTMAXES], F32)
+        nc.scalar.activation(out=log_z_s[:], in_=columns(z_s), func=ACT.Ln)
         total = psum_pair.tile([P, HALVES, PIXELS], F32, tag="pair")
         sums = total[:, 0, 0:SOFTMAXES]
-        nc.tensor.matmul(out=sums, lhsT=ones[:], rhs=expected[:], start=True, stop=False)
-        nc.tensor.matmul(out=sums, lhsT=ones[:], rhs=log_ratio[:], start=False, stop=True)
+        nc.tensor.matmul(out=sums, lhsT=ones[:], rhs=minus_log_z_t[:], start=True, stop=False)
+        nc.tensor.matmul(out=sums, lhsT=ones[:], rhs=expected[:], start=False, stop=False)
+        nc.tensor.matmul(out=sums, lhsT=ones[:], rhs=log_z_s[:], start=False, stop=True)
         scaled = small.tile([P, SOFTMAXES], F32)
         mean = small.tile([P, 1], F32)
         nc.scalar.activation(

@@ -14,6 +14,7 @@ ALU = mybir.AluOpType
 P = 128
 IMAGES = 4
 ALL_IMAGES = 2 * IMAGES
+LAST = ALL_IMAGES - 1
 CHANNELS = 512
 SIDE = 64
 PATCH = 4
@@ -21,6 +22,7 @@ GRID = SIDE // PATCH
 PIXELS = GRID * GRID
 PACK = CHANNELS // P
 HALVES = PIXELS // P
+HALF_PLANE = SIDE * SIDE // HALVES
 ROWS = IMAGES * PIXELS
 SOFTMAXES = IMAGES * HALVES * IMAGES
 INV_TEMPERATURE = 10.0
@@ -29,14 +31,17 @@ NORM_FLOOR_SQUARED = (PATCH * PATCH * 1e-12) ** 2
 ROW_PAIRS = PATCH // 2
 STEPS = PACK * ROW_PAIRS
 POOLING_STEPS = STEPS * ALL_IMAGES
-LOADS_AHEAD = 2
+PLANES_AHEAD = 10
+SCALAR_ITEMS = ()
+CONVERT_LEAD = 2
 
-NORMALISE_DELAY = STEPS
-TURN_BACK_DELAY = STEPS + 3
-QUANTISE_DELAY = STEPS + 8
-RUN_DELAY = STEPS * (IMAGES - 1) + QUANTISE_DELAY + 1 - (IMAGES - 1) ** 2
+NORM_DELAY = 1
+SCALE_DELAY = 2
+TURN_BACK_DELAY = 3
+QUANTISE_DELAY = 6
+NEGATE_DELAY = 8
+PAIR_DELAY = QUANTISE_DELAY + 1
 PRODUCT_LAG = 1
-LAST_STEP = STEPS * IMAGES + RUN_DELAY + IMAGES * IMAGES - 1 + PRODUCT_LAG
 
 FLOPS = 2 * IMAGES * IMAGES * 2 * PIXELS * PIXELS * CHANNELS
 
@@ -45,29 +50,19 @@ def new_pairs(b):
     return [(b, j) for j in range(b + 1)] + [(i, b) for i in range(b)]
 
 
-def quantise_step(k):
-    soonest = STEPS * k + QUANTISE_DELAY
-    return soonest if k < IMAGES else max(soonest, POOLING_STEPS + k % IMAGES)
-
-
-def due(step, delay):
-    k, count = divmod(step - delay, STEPS)
-    return (k, count) if 0 <= k < ALL_IMAGES else (None, None)
-
-
 def tile_criterionminibatchcrossimagepair_kernel(tc, feat_S, feat_T, out):
     nc = tc.nc
     with ExitStack() as ctx:
         const = ctx.enter_context(tc.tile_pool(name="const", bufs=1))
-        raw_pool = ctx.enter_context(tc.tile_pool(name="raw", bufs=LOADS_AHEAD + 1))
-        partial_pool = ctx.enter_context(tc.tile_pool(name="partial", bufs=STEPS))
-        small = ctx.enter_context(tc.tile_pool(name="small", bufs=2))
-        work = ctx.enter_context(tc.tile_pool(name="work", bufs=2))
-        kept = ctx.enter_context(tc.tile_pool(name="kept", bufs=ALL_IMAGES))
+        raw_pool = ctx.enter_context(tc.tile_pool(name="raw", bufs=PLANES_AHEAD + 1))
+        partial_pool = ctx.enter_context(tc.tile_pool(name="partial", bufs=8))
+        converted_pool = ctx.enter_context(tc.tile_pool(name="converted", bufs=2))
+        small = ctx.enter_context(tc.tile_pool(name="small", bufs=4))
+        work = ctx.enter_context(tc.tile_pool(name="work", bufs=4))
+        kept = ctx.enter_context(tc.tile_pool(name="kept", bufs=4))
         unread = ctx.enter_context(tc.tile_pool(name="unread", bufs=4))
         psum_sums = ctx.enter_context(tc.psum_pool(name="psum_sums", bufs=2 * HALVES))
-        psum_back = ctx.enter_context(tc.psum_pool(name="psum_back", bufs=1))
-        psum_pair = ctx.enter_context(tc.psum_pool(name="psum_pair", bufs=3))
+        psum_turn = ctx.enter_context(tc.psum_pool(name="psum_turn", bufs=4))
 
         ident_f32 = const.tile([P, P], F32)
         make_identity(nc, ident_f32[:])
@@ -75,21 +70,25 @@ def tile_criterionminibatchcrossimagepair_kernel(tc, feat_S, feat_T, out):
         make_identity(nc, ident_bf16[:])
         ones = const.tile([P, P], F32)
         nc.vector.memset(ones[:], 1.0)
+        minus_half = const.tile([P, 1], F32)
+        nc.gpsimd.memset(minus_half[:], -0.5)
 
         operands = {}
         for name in ("T", "minus_T", "S"):
             codes = const.tile([P, ROWS], U32, name="codes_" + name, align_bytes=64)
             scales = const.tile([P, ROWS], U8, name="scales_" + name, align_bytes=64)
             operands[name] = {"codes": codes, "scales": scales}
-        z_s = const.tile([P, IMAGES, HALVES, IMAGES], F32)
         z_t = const.tile([P, IMAGES, HALVES, IMAGES], F32)
-        cross = const.tile([P, IMAGES, HALVES, IMAGES], F32)
-        inv_z = const.tile([P, SOFTMAXES], F32)
+        inv_z = const.tile([P, IMAGES, HALVES, IMAGES], F32)
+        z_s = const.tile([P, IMAGES, HALVES, IMAGES + 1], F32)
+        cross = const.tile([P, IMAGES, HALVES, IMAGES + 1], F32)
 
-        exp_t = const.tile([P, IMAGES * IMAGES, HALVES, PIXELS], F32)
+        exp_t = const.tile([P, IMAGES, IMAGES, HALVES, PIXELS], F32)
 
         raw = {}
+        converted = {}
         by_pixel = {}
+        inv_norm = {}
         unit = {}
         grouped = {}
         dif = {}
@@ -97,110 +96,127 @@ def tile_criterionminibatchcrossimagepair_kernel(tc, feat_S, feat_T, out):
         def is_teacher(k):
             return k < IMAGES
 
-        def columns(per_softmax):
-            return per_softmax[:].rearrange("p i h j -> p (i h j)")
-
-        def load(k):
+        def load(k, j, halves):
             feat = feat_T if is_teacher(k) else feat_S
-            planes = feat[k % IMAGES].rearrange("(p j) h w -> p j (h w)", j=PACK)
-            raw[k] = raw_pool.tile([P, PACK, SIDE * SIDE], BF16, name="raw")
-            for j in range(PACK):
-                nc.sync.dma_start(out=raw[k][:, j, :], in_=planes[:, j, :])
+            plane = feat[k % IMAGES].rearrange("(p j) h w -> p j (h w)", j=PACK)[:, j, :]
+            if halves[0] == 0:
+                raw[k, j] = raw_pool.tile([P, SIDE * SIDE], BF16, name="raw")
+            span = slice(halves[0] * HALF_PLANE, (halves[-1] + 1) * HALF_PLANE)
+            nc.sync.dma_start(out=raw[k, j][:, span], in_=plane[:, span])
 
-        def add_rows(k, count):
-            j, dy = divmod(count, ROW_PAIRS)
-            if count == 0:
-                by_pixel[k] = [
-                    psum_sums.tile([P, PACK, P], F32, name="by_pixel") for half in range(HALVES)
-                ]
-            places = raw[k][:, j, :].rearrange(
+        def places(k, j, halves):
+            span = slice(halves[0] * HALF_PLANE, (halves[-1] + 1) * HALF_PLANE)
+            return raw[k, j][:, span].rearrange(
                 "p (y dy x dx) -> p dy dx y x", dy=PATCH, x=GRID, dx=PATCH
             )
-            partial = partial_pool.tile([P, PATCH, PIXELS], F32)
-            nc.vector.tensor_tensor(
-                out=partial[:].rearrange("p dx (y x) -> p dx y x", x=GRID),
-                in0=places[:, dy],
-                in1=places[:, dy + ROW_PAIRS],
-                op=ALU.add,
-            )
-            for half in range(HALVES):
+
+        def turn(k, j, halves, partial, first, last):
+            for position, half in enumerate(halves):
+                if j == 0 and first:
+                    by_pixel[k, half] = psum_sums.tile([P, PACK, P], F32, tag="sums", name="by_pixel")
                 for dx in range(PATCH):
                     nc.tensor.matmul(
-                        out=by_pixel[k][half][:, j, :],
-                        lhsT=partial[:, dx, half * P : (half + 1) * P],
+                        out=by_pixel[k, half][:, j, :],
+                        lhsT=partial[:, dx, position * P : (position + 1) * P],
                         rhs=ident_f32[:],
                         is_transpose=True,
-                        start=(dy == 0 and dx == 0),
-                        stop=(dy == ROW_PAIRS - 1 and dx == PATCH - 1),
+                        start=(first and dx == 0),
+                        stop=(last and dx == PATCH - 1),
                     )
 
-        def normalise(k):
-            square_sum = small.tile([P, HALVES], F32)
-            for half in range(HALVES):
-                squares = unread.tile([P, CHANNELS], F32)
-                nc.scalar.activation(
-                    out=squares[:],
-                    in_=by_pixel[k][half][:].rearrange("n j p -> n (j p)"),
-                    func=ACT.Square,
-                    accum_out=square_sum[:, half : half + 1],
-                )
-            above_floor = small.tile([P, HALVES], F32)
-            nc.scalar.activation(out=above_floor[:], in_=square_sum[:], func=ACT.Relu, bias=-NORM_FLOOR_SQUARED)
-            inv_norm = small.tile([P, HALVES], F32)
-            nc.scalar.activation(
-                out=inv_norm[:], in_=above_floor[:], func=ACT.Abs_reciprocal_sqrt, bias=NORM_FLOOR_SQUARED
+        def add_rows(k, j, dy, halves):
+            source = places(k, j, halves)
+            partial = partial_pool.tile([P, PATCH, len(halves) * P], F32)
+            nc.vector.tensor_tensor(
+                out=partial[:].rearrange("p dx (y x) -> p dx y x", x=GRID),
+                in0=source[:, dy],
+                in1=source[:, dy + ROW_PAIRS],
+                op=ALU.add,
             )
-            unit[k] = work.tile([P, HALVES, CHANNELS], BF16, name="unit")
-            for half in range(HALVES):
-                nc.scalar.activation(
-                    out=unit[k][:, half, :],
-                    in_=by_pixel[k][half][:].rearrange("n j p -> n (j p)"),
-                    func=ACT.Copy,
-                    scale=inv_norm[:, half : half + 1],
-                )
+            turn(k, j, halves, partial, dy == 0, dy == ROW_PAIRS - 1)
 
-        def turn_back(k):
-            back = psum_back.tile([P, PACK, PIXELS], BF16)
-            for half in range(HALVES):
+        def convert(k, j, dy):
+            converted[k, j, dy] = []
+            for row in (dy, dy + ROW_PAIRS):
+                tile = converted_pool.tile([P, PATCH, PIXELS], F32, name="converted")
+                nc.scalar.copy(
+                    out=tile[:].rearrange("p dx (y x) -> p dx y x", x=GRID),
+                    in_=places(k, j, (0, 1))[:, row],
+                )
+                converted[k, j, dy].append(tile)
+
+        def turn_converted(k, j, dy):
+            for number, tile in enumerate(converted[k, j, dy]):
+                turn(k, j, (0, 1), tile, dy == 0 and number == 0, dy == ROW_PAIRS - 1 and number == 1)
+
+        def norm(k, half):
+            square_sum = small.tile([P, 1], F32)
+            squares = unread.tile([P, CHANNELS], F32)
+            nc.scalar.activation(
+                out=squares[:],
+                in_=by_pixel[k, half][:].rearrange("n j p -> n (j p)"),
+                func=ACT.Square,
+                accum_out=square_sum[:],
+            )
+            floored = small.tile([P, 1], F32)
+            nc.gpsimd.tensor_scalar(
+                out=floored[:], in0=square_sum[:], scalar1=NORM_FLOOR_SQUARED, scalar2=None, op0=ALU.max
+            )
+            inv_norm[k, half] = small.tile([P, 1], F32, name="inv_norm")
+            nc.gpsimd.tensor_tensor(out=inv_norm[k, half][:], in0=floored[:], in1=minus_half[:], op=ALU.pow)
+
+        def scale_to_unit(k, half):
+            unit[k, half] = work.tile([P, CHANNELS], BF16, name="unit")
+            nc.scalar.activation(
+                out=unit[k, half][:],
+                in_=by_pixel[k, half][:].rearrange("n j p -> n (j p)"),
+                func=ACT.Copy,
+                scale=inv_norm[k, half][:],
+            )
+
+        def turn_back(k, halves):
+            back = psum_turn.tile([P, len(halves), PACK, P], BF16, tag="turn", name="back")
+            for position, half in enumerate(halves):
                 for j in range(PACK):
                     nc.tensor.transpose(
-                        back[:, j, half * P : (half + 1) * P],
-                        unit[k][:, half, j * P : (j + 1) * P],
-                        ident_bf16[:],
+                        back[:, position, j, :], unit[k, half][:, j * P : (j + 1) * P], ident_bf16[:]
                     )
-            grouped[k] = kept.tile([P, PIXELS, PACK], BF16, name="grouped", align_bytes=64)
-            nc.scalar.copy(out=grouped[k][:], in_=back[:].rearrange("p j n -> p n j"))
+            for position, half in enumerate(halves):
+                grouped[k, half] = kept.tile([P, P, PACK], BF16, name="grouped", align_bytes=64)
+                nc.scalar.copy(out=grouped[k, half][:], in_=back[:, position].rearrange("p j n -> p n j"))
 
-        def quantise_as(name, b, values):
-            cols = slice(b * PIXELS, (b + 1) * PIXELS)
+        def quantise_as(name, b, half, values):
+            cols = slice(b * PIXELS + half * P, b * PIXELS + (half + 1) * P)
             nc.vector.quantize_mx(
                 out=operands[name]["codes"][:, cols].bitcast(FP8X4),
                 scales=operands[name]["scales"][:, cols],
                 in_=values[:].rearrange("p n j -> p (n j)"),
             )
 
-        def quantise(k):
-            quantise_as("T" if is_teacher(k) else "S", k % IMAGES, grouped[k])
+        def quantise(k, half):
+            quantise_as("T" if is_teacher(k) else "S", k % IMAGES, half, grouped[k, half])
 
         def quantise_negated(k):
-            negated = work.tile([P, PIXELS, PACK], BF16, align_bytes=64)
-            nc.vector.tensor_scalar_mul(out=negated[:], in0=grouped[k][:], scalar1=-1.0)
-            quantise_as("minus_T", k, negated)
-
-        def similarity(acc, passes, i, j):
-            cols = slice(j * PIXELS, (j + 1) * PIXELS)
+            negated = {}
             for half in range(HALVES):
-                rows = slice(i * PIXELS + half * P, i * PIXELS + (half + 1) * P)
-                for number, (left, right) in enumerate(passes):
-                    nc.tensor.matmul_mx(
-                        out=acc[:, half, :],
-                        lhsT=operands[left]["codes"][:, rows].bitcast(FP8X4),
-                        lhsT_scale=operands[left]["scales"][:, rows],
-                        rhs=operands[right]["codes"][:, cols].bitcast(FP8X4),
-                        rhs_scale=operands[right]["scales"][:, cols],
-                        start=(number == 0),
-                        stop=(number == len(passes) - 1),
-                    )
+                negated[half] = work.tile([P, P, PACK], BF16, name="negated", align_bytes=64)
+                nc.vector.tensor_scalar_mul(out=negated[half][:], in0=grouped[k, half][:], scalar1=-1.0)
+            for half in range(HALVES):
+                quantise_as("minus_T", k, half, negated[half])
+
+        def similarity(acc, passes, i, half, j, cols):
+            rows = slice(i * PIXELS + half * P, i * PIXELS + (half + 1) * P)
+            span = slice(j * PIXELS + cols.start, j * PIXELS + cols.stop)
+            for number, (left, right) in enumerate(passes):
+                nc.tensor.matmul_mx(
+                    out=acc,
+                    lhsT=operands[left]["codes"][:, rows].bitcast(FP8X4),
+                    lhsT_scale=operands[left]["scales"][:, rows],
+                    rhs=operands[right]["codes"][:, span].bitcast(FP8X4),
+                    rhs_scale=operands[right]["scales"][:, span],
+                    start=(number == 0),
+                    stop=(number == len(passes) - 1),
+                )
 
         def shifted_exp(result, sim, row_sum):
             nc.scalar.activation(
@@ -208,81 +224,157 @@ def tile_criterionminibatchcrossimagepair_kernel(tc, feat_S, feat_T, out):
                 accum_out=row_sum,
             )
 
-        def teacher_pair(number, i, j):
-            sim = psum_pair.tile([P, HALVES, PIXELS], F32, tag="pair")
-            similarity(sim, (("T", "T"),), i, j)
+        def teacher_pair(i, j):
+            sim = psum_turn.tile([P, HALVES, PIXELS], F32, tag="turn", name="sim_t")
             for half in range(HALVES):
-                shifted_exp(exp_t[:, number, half, :], sim[:, half, :], z_t[:, i, half, j : j + 1])
+                similarity(sim[:, half, :], (("T", "T"),), i, half, j, slice(0, PIXELS))
+            for half in range(HALVES):
+                shifted_exp(exp_t[:, i, j, half, :], sim[:, half, :], z_t[:, i, half, j : j + 1])
 
-        def student_pair(number, i, j):
-            dif[number] = psum_pair.tile([P, HALVES, PIXELS], F32, tag="pair", name="dif")
-            similarity(dif[number], (("S", "S"), ("T", "minus_T")), i, j)
-            sim = psum_pair.tile([P, HALVES, PIXELS], F32, tag="pair")
-            similarity(sim, (("S", "S"),), i, j)
-            for half in range(HALVES):
+        def student_sims(blocks):
+            sim = psum_turn.tile([P, HALVES * PIXELS], F32, tag="turn", name="sim_s")
+            at = 0
+            spans = []
+            for i, half, j, cols, slot in blocks:
+                width = cols.stop - cols.start
+                spans.append(slice(at, at + width))
+                at += width
+            for (i, half, j, cols, slot), span in zip(blocks, spans):
+                similarity(sim[:, span], (("S", "S"),), i, half, j, cols)
+            for (i, half, j, cols, slot), span in zip(blocks, spans):
                 exp_s = unread.tile([P, PIXELS], F32)
-                shifted_exp(exp_s[:], sim[:, half, :], z_s[:, i, half, j : j + 1])
+                shifted_exp(exp_s[:, 0 : cols.stop - cols.start], sim[:, span], z_s[:, i, half, slot : slot + 1])
 
-        def product(number, i, j):
-            for half in range(HALVES):
+        def student_difs(key, blocks, pool=psum_turn):
+            dif[key] = pool.tile([P, HALVES * PIXELS], F32, tag="sums" if pool is psum_sums else "turn", name="dif")
+            at = 0
+            for i, half, j, cols, slot in blocks:
+                width = cols.stop - cols.start
+                similarity(dif[key][:, at : at + width], (("S", "S"), ("T", "minus_T")), i, half, j, cols)
+                at += width
+
+        def products(key, blocks):
+            at = 0
+            for i, half, j, cols, slot in blocks:
+                width = cols.stop - cols.start
                 weighted = unread.tile([P, PIXELS], F32)
                 nc.vector.scalar_tensor_tensor(
-                    out=weighted[:],
-                    in0=dif[number][:, half, :],
+                    out=weighted[:, 0:width],
+                    in0=dif[key][:, at : at + width],
                     scalar=-INV_TEMPERATURE,
-                    in1=exp_t[:, number, half, :],
+                    in1=exp_t[:, i, j, half, cols],
                     op0=ALU.mult,
                     op1=ALU.mult,
-                    accum_out=cross[:, i, half, j : j + 1],
+                    accum_out=cross[:, i, half, slot : slot + 1],
                 )
+                at += width
 
+        plan = {}
+
+        def at_step(step, rank, call, *args):
+            plan.setdefault((step, rank), []).append((call, args))
+
+        both = (0, 1)
+        loads = [(k, j, both) for k in range(LAST) for j in range(PACK)]
+        loads += [(LAST, j, (half,)) for half in both for j in range(PACK)]
+        for number, args in enumerate(loads):
+            at_step(0 if number < PLANES_AHEAD else 2 * (number - PLANES_AHEAD), 0.5, load, *args)
+        for k in range(LAST):
+            for count in range(STEPS):
+                j, dy = divmod(count, ROW_PAIRS)
+                step = STEPS * k + count
+                if (k, j, dy) in SCALAR_ITEMS:
+                    at_step(step - CONVERT_LEAD, 0.7, convert, k, j, dy)
+                    at_step(step, 1, turn_converted, k, j, dy)
+                else:
+                    at_step(step, 1, add_rows, k, j, dy, both)
+            done = STEPS * k + STEPS - 1
+            for half in both:
+                at_step(done + NORM_DELAY, 3, norm, k, half)
+                at_step(done + SCALE_DELAY, 3, scale_to_unit, k, half)
+            at_step(done + TURN_BACK_DELAY, 3, turn_back, k, both)
+            for half in both:
+                at_step(done + QUANTISE_DELAY, 3, quantise, k, half)
+            if is_teacher(k):
+                at_step(done + NEGATE_DELAY, 3, quantise_negated, k)
+            for count, (i, j) in enumerate(new_pairs(k % IMAGES)):
+                step = done + PAIR_DELAY + count
+                if is_teacher(k):
+                    at_step(step, 0, teacher_pair, i, j)
+                else:
+                    blocks = [(i, half, j, slice(0, PIXELS), j) for half in both]
+                    at_step(step, 0, student_difs, (i, j), blocks)
+                    at_step(step, 0, student_sims, blocks)
+                    at_step(step + PRODUCT_LAG, 2, products, (i, j), blocks)
+        at_step(POOLING_STEPS - 2, 2.5, nc.vector.reciprocal, inv_z[:].rearrange("p i h j -> p (i h j)"), z_t[:].rearrange("p i h j -> p (i h j)"))
+
+        for half in both:
+            for j in range(PACK):
+                for dy in range(ROW_PAIRS):
+                    at_step(STEPS * LAST + half * PACK + j, 1, add_rows, LAST, j, dy, (half,))
+        b = LAST % IMAGES
+        lo, hi = slice(0, P), slice(P, PIXELS)
+        end = POOLING_STEPS
+        before = end - PACK
+        at_step(before, 3, norm, LAST, 0)
+        at_step(before + 1, 3, scale_to_unit, LAST, 0)
+        at_step(before + 2, 3, turn_back, LAST, (0,))
+        at_step(end - 1, 2.8, quantise, LAST, 0)
+        whole = slice(0, PIXELS)
+        early = [
+            [(b, 0, 0, whole, 0), (b, 0, 1, whole, 1)],
+            [(b, 0, 2, whole, 2), (b, 0, b, lo, b)],
+            [(0, 0, b, lo, b), (0, 1, b, lo, b), (1, 0, b, lo, b), (1, 1, b, lo, b)],
+            [(2, 0, b, lo, b), (2, 1, b, lo, b)],
+        ]
+        late = [
+            [(b, 1, 0, whole, 0), (b, 1, 1, whole, 1)],
+            [(b, 1, 2, whole, 2), (b, 1, b, whole, b)],
+            [(0, 0, b, hi, IMAGES), (0, 1, b, hi, IMAGES), (1, 0, b, hi, IMAGES), (1, 1, b, hi, IMAGES)],
+            [(2, 0, b, hi, IMAGES), (2, 1, b, hi, IMAGES), (b, 0, b, hi, IMAGES)],
+        ]
+        pending = [early[0], early[1], early[2], early[3]]
+        seq = [
+            (norm, LAST, 1),
+            (student_difs, "e0", early[0], psum_sums), (student_sims, early[0]),
+            (scale_to_unit, LAST, 1),
+            (products, "e0", early[0]),
+            (student_difs, "e1", early[1], psum_turn), (student_sims, early[1]),
+            (turn_back, LAST, (1,)),
+            (products, "e1", early[1]),
+            (quantise, LAST, 1),
+            (student_difs, "e2", early[2], psum_sums), (student_sims, early[2]), (products, "e2", early[2]),
+            (student_difs, "e3", early[3], psum_turn), (student_sims, early[3]), (products, "e3", early[3]),
+            (student_sims, late[0]), (student_difs, "l0", late[0], psum_sums), (products, "l0", late[0]),
+            (student_sims, late[1]), (student_difs, "l1", late[1], psum_sums), (products, "l1", late[1]),
+            (student_sims, late[2]), (student_difs, "l2", late[2], psum_sums), (products, "l2", late[2]),
+            (student_sims, late[3]), (student_difs, "l3", late[3], psum_sums), (products, "l3", late[3]),
+        ]
+        for number, entry in enumerate(seq):
+            at_step(end + number, 0, entry[0], *entry[1:])
+        nc.vector.memset(z_s[:], 0.0)
+        nc.vector.memset(cross[:], 0.0)
         ctx.enter_context(tc.manual_schedule())
-        pairs = [pair for b in range(IMAGES) for pair in new_pairs(b)]
-        for k in range(LOADS_AHEAD):
-            load(k)
-        for step in range(LAST_STEP + 1):
-            k, count = due(step, 0)
-            if k is not None:
-                if count == 0 and k + LOADS_AHEAD < ALL_IMAGES:
-                    load(k + LOADS_AHEAD)
-                add_rows(k, count)
-            for stage, delay in ((normalise, NORMALISE_DELAY), (turn_back, TURN_BACK_DELAY)):
-                k, count = due(step, delay)
-                if count == 0:
-                    stage(k)
-            for k in range(ALL_IMAGES):
-                if step == quantise_step(k):
-                    quantise(k)
-            k = step - POOLING_STEPS
-            if 0 <= k < IMAGES:
-                quantise_negated(k)
-            if k == IMAGES:
-                nc.vector.reciprocal(out=inv_z[:], in_=columns(z_t))
-            number = step - RUN_DELAY
-            if 0 <= number < len(pairs):
-                teacher_pair(number, *pairs[number])
-            number = step - RUN_DELAY - STEPS * IMAGES
-            if 0 <= number < len(pairs):
-                student_pair(number, *pairs[number])
-            number = number - PRODUCT_LAG
-            if 0 <= number < len(pairs):
-                product(number, *pairs[number])
+        for key in sorted(plan):
+            for call, args in plan[key]:
+                call(*args)
 
-        expected = small.tile([P, SOFTMAXES], F32)
-        nc.vector.tensor_mul(out=expected[:], in0=columns(cross), in1=inv_z[:])
-        minus_log_z_t = small.tile([P, SOFTMAXES], F32)
-        nc.scalar.activation(out=minus_log_z_t[:], in_=inv_z[:], func=ACT.Ln)
-        log_z_s = small.tile([P, SOFTMAXES], F32)
-        nc.scalar.activation(out=log_z_s[:], in_=columns(z_s), func=ACT.Ln)
-        total = psum_pair.tile([P, HALVES, PIXELS], F32, tag="pair")
-        sums = total[:, 0, 0:SOFTMAXES]
-        nc.tensor.matmul(out=sums, lhsT=ones[:], rhs=minus_log_z_t[:], start=True, stop=False)
-        nc.tensor.matmul(out=sums, lhsT=ones[:], rhs=expected[:], start=False, stop=False)
-        nc.tensor.matmul(out=sums, lhsT=ones[:], rhs=log_z_s[:], start=False, stop=True)
-        scaled = small.tile([P, SOFTMAXES], F32)
+        nc.vector.tensor_add(out=z_s[:, :, :, b], in0=z_s[:, :, :, b], in1=z_s[:, :, :, IMAGES])
+        nc.vector.tensor_add(out=cross[:, :, :, b], in0=cross[:, :, :, b], in1=cross[:, :, :, IMAGES])
+        ratio = small.tile([P, IMAGES * HALVES, IMAGES], F32)
+        inv_z_rows = inv_z[:].rearrange("p i h j -> p (i h) j")
+        nc.vector.tensor_mul(out=ratio[:], in0=z_s[:].rearrange("p i h j -> p (i h) j")[:, :, 0:IMAGES], in1=inv_z_rows)
+        row_sums = small.tile([P, 2], F32)
+        expected = small.tile([P, IMAGES * HALVES, IMAGES], F32)
+        nc.vector.scalar_tensor_tensor(out=expected[:], in0=cross[:].rearrange("p i h j -> p (i h) j")[:, :, 0:IMAGES], scalar=1.0, in1=inv_z_rows, op0=ALU.mult, op1=ALU.mult, accum_out=row_sums[:, 0:1])
+        log_ratio = small.tile([P, SOFTMAXES], F32)
+        nc.scalar.activation(out=log_ratio[:], in_=ratio[:].rearrange("p r j -> p (r j)"), func=ACT.Ln, accum_out=row_sums[:, 1:2])
+        total = psum_turn.tile([P, HALVES * PIXELS], F32, tag="turn", name="total")
+        nc.tensor.matmul(out=total[:, 0:2], lhsT=ones[:], rhs=row_sums[:], start=True, stop=True)
+        scaled = small.tile([P, 2], F32)
         mean = small.tile([P, 1], F32)
         nc.scalar.activation(
-            out=scaled[:], in_=sums, func=ACT.Copy, scale=1.0 / (IMAGES * IMAGES * PIXELS), accum_out=mean[:]
+            out=scaled[:], in_=total[:, 0:2], func=ACT.Copy, scale=1.0 / (IMAGES * IMAGES * PIXELS), accum_out=mean[:]
         )
         out_view = out
         for axis in range(2 - len(out.shape)):

@@ -37,9 +37,9 @@ CONVERT_LEAD = 2
 
 NORM_DELAY = 1
 SCALE_DELAY = 2
-TURN_BACK_DELAY = 3
-QUANTISE_DELAY = 6
-NEGATE_DELAY = 8
+TURN_BACK_DELAY = 6
+QUANTISE_DELAY = 9
+NEGATE_DELAY = 11
 PAIR_DELAY = QUANTISE_DELAY + 1
 PRODUCT_LAG = 1
 
@@ -70,8 +70,6 @@ def tile_criterionminibatchcrossimagepair_kernel(tc, feat_S, feat_T, out):
         make_identity(nc, ident_bf16[:])
         ones = const.tile([P, P], F32)
         nc.vector.memset(ones[:], 1.0)
-        minus_half = const.tile([P, 1], F32)
-        nc.gpsimd.memset(minus_half[:], -0.5)
 
         operands = {}
         for name in ("T", "minus_T", "S"):
@@ -149,21 +147,27 @@ def tile_criterionminibatchcrossimagepair_kernel(tc, feat_S, feat_T, out):
             for number, tile in enumerate(converted[k, j, dy]):
                 turn(k, j, (0, 1), tile, dy == 0 and number == 0, dy == ROW_PAIRS - 1 and number == 1)
 
-        def norm(k, half):
-            square_sum = small.tile([P, 1], F32)
-            squares = unread.tile([P, CHANNELS], F32)
+        def norm(k, halves):
+            square_sum = small.tile([P, HALVES], F32)
+            for half in halves:
+                squares = unread.tile([P, CHANNELS], F32)
+                nc.scalar.activation(
+                    out=squares[:],
+                    in_=by_pixel[k, half][:].rearrange("n j p -> n (j p)"),
+                    func=ACT.Square,
+                    accum_out=square_sum[:, half : half + 1],
+                )
+            span = slice(halves[0], halves[-1] + 1)
+            above_floor = small.tile([P, HALVES], F32)
             nc.scalar.activation(
-                out=squares[:],
-                in_=by_pixel[k, half][:].rearrange("n j p -> n (j p)"),
-                func=ACT.Square,
-                accum_out=square_sum[:],
+                out=above_floor[:, span], in_=square_sum[:, span], func=ACT.Relu, bias=-NORM_FLOOR_SQUARED
             )
-            floored = small.tile([P, 1], F32)
-            nc.gpsimd.tensor_scalar(
-                out=floored[:], in0=square_sum[:], scalar1=NORM_FLOOR_SQUARED, scalar2=None, op0=ALU.max
+            inverse = small.tile([P, HALVES], F32)
+            nc.scalar.activation(
+                out=inverse[:, span], in_=above_floor[:, span], func=ACT.Abs_reciprocal_sqrt, bias=NORM_FLOOR_SQUARED
             )
-            inv_norm[k, half] = small.tile([P, 1], F32, name="inv_norm")
-            nc.gpsimd.tensor_tensor(out=inv_norm[k, half][:], in0=floored[:], in1=minus_half[:], op=ALU.pow)
+            for half in halves:
+                inv_norm[k, half] = inverse[:, half : half + 1]
 
         def scale_to_unit(k, half):
             unit[k, half] = work.tile([P, CHANNELS], BF16, name="unit")
@@ -171,7 +175,7 @@ def tile_criterionminibatchcrossimagepair_kernel(tc, feat_S, feat_T, out):
                 out=unit[k, half][:],
                 in_=by_pixel[k, half][:].rearrange("n j p -> n (j p)"),
                 func=ACT.Copy,
-                scale=inv_norm[k, half][:],
+                scale=inv_norm[k, half],
             )
 
         def turn_back(k, halves):
@@ -289,8 +293,8 @@ def tile_criterionminibatchcrossimagepair_kernel(tc, feat_S, feat_T, out):
                 else:
                     at_step(step, 1, add_rows, k, j, dy, both)
             done = STEPS * k + STEPS - 1
+            at_step(done + NORM_DELAY, 3, norm, k, both)
             for half in both:
-                at_step(done + NORM_DELAY, 3, norm, k, half)
                 at_step(done + SCALE_DELAY, 3, scale_to_unit, k, half)
             at_step(done + TURN_BACK_DELAY, 3, turn_back, k, both)
             for half in both:
@@ -316,7 +320,7 @@ def tile_criterionminibatchcrossimagepair_kernel(tc, feat_S, feat_T, out):
         lo, hi = slice(0, P), slice(P, PIXELS)
         end = POOLING_STEPS
         before = end - PACK
-        at_step(before, 3, norm, LAST, 0)
+        at_step(before, 3, norm, LAST, (0,))
         at_step(before + 1, 3, scale_to_unit, LAST, 0)
         at_step(before + 2, 3, turn_back, LAST, (0,))
         at_step(end - 1, 2.8, quantise, LAST, 0)
@@ -335,7 +339,7 @@ def tile_criterionminibatchcrossimagepair_kernel(tc, feat_S, feat_T, out):
         ]
         pending = [early[0], early[1], early[2], early[3]]
         seq = [
-            (norm, LAST, 1),
+            (norm, LAST, (1,)),
             (student_difs, "e0", early[0], psum_sums), (student_sims, early[0]),
             (scale_to_unit, LAST, 1),
             (products, "e0", early[0]),

@@ -33,14 +33,12 @@ STEPS = PACK * ROW_PAIRS
 POOLING_STEPS = STEPS * ALL_IMAGES
 PLANES_AHEAD = 10
 SCALAR_ITEMS = ()
-CONVERT_LEAD = 2
+CONVERT_LEAD = 4
+LAST_LEAD = 2
+LAST_ITEMS = ()
+DELAYS = [(1,2,6,9,10,1)]*5+[(1,1,4,8,9,2),(2,2,4,7,0,1)]
 
-NORM_DELAY = 1
-SCALE_DELAY = 2
-TURN_BACK_DELAY = 6
-QUANTISE_DELAY = 9
 NEGATE_DELAY = 11
-PAIR_DELAY = QUANTISE_DELAY + 1
 PRODUCT_LAG = 1
 
 FLOPS = 2 * IMAGES * IMAGES * 2 * PIXELS * PIXELS * CHANNELS
@@ -56,8 +54,8 @@ def tile_criterionminibatchcrossimagepair_kernel(tc, feat_S, feat_T, out):
         const = ctx.enter_context(tc.tile_pool(name="const", bufs=1))
         raw_pool = ctx.enter_context(tc.tile_pool(name="raw", bufs=PLANES_AHEAD + 1))
         partial_pool = ctx.enter_context(tc.tile_pool(name="partial", bufs=8))
-        converted_pool = ctx.enter_context(tc.tile_pool(name="converted", bufs=2))
-        small = ctx.enter_context(tc.tile_pool(name="small", bufs=4))
+        converted_pool = ctx.enter_context(tc.tile_pool(name="converted", bufs=4))
+        small = ctx.enter_context(tc.tile_pool(name="small", bufs=6))
         work = ctx.enter_context(tc.tile_pool(name="work", bufs=4))
         kept = ctx.enter_context(tc.tile_pool(name="kept", bufs=4))
         unread = ctx.enter_context(tc.tile_pool(name="unread", bufs=4))
@@ -66,8 +64,6 @@ def tile_criterionminibatchcrossimagepair_kernel(tc, feat_S, feat_T, out):
 
         ident_f32 = const.tile([P, P], F32)
         make_identity(nc, ident_f32[:])
-        ident_bf16 = const.tile([P, P], BF16)
-        make_identity(nc, ident_bf16[:])
         ones = const.tile([P, P], F32)
         nc.vector.memset(ones[:], 1.0)
 
@@ -78,8 +74,8 @@ def tile_criterionminibatchcrossimagepair_kernel(tc, feat_S, feat_T, out):
             operands[name] = {"codes": codes, "scales": scales}
         z_t = const.tile([P, IMAGES, HALVES, IMAGES], F32)
         inv_z = const.tile([P, IMAGES, HALVES, IMAGES], F32)
-        z_s = const.tile([P, IMAGES, HALVES, IMAGES + 1], F32)
-        cross = const.tile([P, IMAGES, HALVES, IMAGES + 1], F32)
+        z_s = const.tile([P, IMAGES, HALVES, IMAGES], F32)
+        cross = const.tile([P, IMAGES, HALVES, IMAGES], F32)
 
         exp_t = const.tile([P, IMAGES, IMAGES, HALVES, PIXELS], F32)
 
@@ -123,29 +119,32 @@ def tile_criterionminibatchcrossimagepair_kernel(tc, feat_S, feat_T, out):
                     )
 
         def add_rows(k, j, dy, halves):
-            source = places(k, j, halves)
-            partial = partial_pool.tile([P, PATCH, len(halves) * P], F32)
-            nc.vector.tensor_tensor(
-                out=partial[:].rearrange("p dx (y x) -> p dx y x", x=GRID),
-                in0=source[:, dy],
-                in1=source[:, dy + ROW_PAIRS],
-                op=ALU.add,
-            )
+            partial = partial_pool.tile([P, PATCH, len(halves) * P], F32, name="partial")
+            parts = [(half,) for half in halves] if k == 0 and j == 0 else [halves]
+            for part in parts:
+                source = places(k, j, part)
+                at = (part[0] - halves[0]) * P
+                nc.vector.tensor_tensor(
+                    out=partial[:, :, at : at + len(part) * P].rearrange("p dx (y x) -> p dx y x", x=GRID),
+                    in0=source[:, dy],
+                    in1=source[:, dy + ROW_PAIRS],
+                    op=ALU.add,
+                )
             turn(k, j, halves, partial, dy == 0, dy == ROW_PAIRS - 1)
 
-        def convert(k, j, dy):
-            converted[k, j, dy] = []
+        def convert(k, j, dy, halves=(0, 1)):
+            converted[k, j, dy, halves] = []
             for row in (dy, dy + ROW_PAIRS):
-                tile = converted_pool.tile([P, PATCH, PIXELS], F32, name="converted")
+                tile = converted_pool.tile([P, PATCH, len(halves) * P], F32, name="converted")
                 nc.scalar.copy(
                     out=tile[:].rearrange("p dx (y x) -> p dx y x", x=GRID),
-                    in_=places(k, j, (0, 1))[:, row],
+                    in_=places(k, j, halves)[:, row],
                 )
-                converted[k, j, dy].append(tile)
+                converted[k, j, dy, halves].append(tile)
 
-        def turn_converted(k, j, dy):
-            for number, tile in enumerate(converted[k, j, dy]):
-                turn(k, j, (0, 1), tile, dy == 0 and number == 0, dy == ROW_PAIRS - 1 and number == 1)
+        def turn_converted(k, j, dy, halves=(0, 1)):
+            for number, tile in enumerate(converted[k, j, dy, halves]):
+                turn(k, j, halves, tile, dy == 0 and number == 0, dy == ROW_PAIRS - 1 and number == 1)
 
         def norm(k, halves):
             square_sum = small.tile([P, HALVES], F32)
@@ -172,29 +171,31 @@ def tile_criterionminibatchcrossimagepair_kernel(tc, feat_S, feat_T, out):
         def scale_to_unit(k, half):
             unit[k, half] = work.tile([P, CHANNELS], BF16, name="unit")
             nc.scalar.activation(
-                out=unit[k, half][:],
-                in_=by_pixel[k, half][:].rearrange("n j p -> n (j p)"),
+                out=unit[k, half][:].rearrange("n (u p e) -> n u p e", u=2, e=2),
+                in_=by_pixel[k, half][:].rearrange("n (u e) p -> n u p e", e=2),
                 func=ACT.Copy,
                 scale=inv_norm[k, half],
             )
 
         def turn_back(k, halves):
-            back = psum_turn.tile([P, len(halves), PACK, P], BF16, tag="turn", name="back")
+            back = psum_turn.tile([P, len(halves), 2, P], F32, tag="turn", name="back")
             for position, half in enumerate(halves):
-                for j in range(PACK):
-                    nc.tensor.transpose(
-                        back[:, position, j, :], unit[k, half][:, j * P : (j + 1) * P], ident_bf16[:]
-                    )
+                words = unit[k, half][:].bitcast(F32)
+                for u in range(2):
+                    nc.tensor.transpose(back[:, position, u, :], words[:, u * P : (u + 1) * P], ident_f32[:])
             for position, half in enumerate(halves):
-                grouped[k, half] = kept.tile([P, P, PACK], BF16, name="grouped", align_bytes=64)
-                nc.scalar.copy(out=grouped[k, half][:], in_=back[:, position].rearrange("p j n -> p n j"))
+                grouped[k, half] = kept.tile([P, P * PACK], BF16, name="grouped", align_bytes=64)
+                nc.scalar.copy(
+                    out=grouped[k, half][:].bitcast(F32).rearrange("p (n u) -> p n u", u=2),
+                    in_=back[:, position].rearrange("p u n -> p n u"),
+                )
 
         def quantise_as(name, b, half, values):
             cols = slice(b * PIXELS + half * P, b * PIXELS + (half + 1) * P)
             nc.vector.quantize_mx(
                 out=operands[name]["codes"][:, cols].bitcast(FP8X4),
                 scales=operands[name]["scales"][:, cols],
-                in_=values[:].rearrange("p n j -> p (n j)"),
+                in_=values[:],
             )
 
         def quantise(k, half):
@@ -203,7 +204,7 @@ def tile_criterionminibatchcrossimagepair_kernel(tc, feat_S, feat_T, out):
         def quantise_negated(k):
             negated = {}
             for half in range(HALVES):
-                negated[half] = work.tile([P, P, PACK], BF16, name="negated", align_bytes=64)
+                negated[half] = work.tile([P, P * PACK], BF16, name="negated", align_bytes=64)
                 nc.vector.tensor_scalar_mul(out=negated[half][:], in0=grouped[k, half][:], scalar1=-1.0)
             for half in range(HALVES):
                 quantise_as("minus_T", k, half, negated[half])
@@ -279,7 +280,7 @@ def tile_criterionminibatchcrossimagepair_kernel(tc, feat_S, feat_T, out):
             plan.setdefault((step, rank), []).append((call, args))
 
         both = (0, 1)
-        loads = [(k, j, both) for k in range(LAST) for j in range(PACK)]
+        loads = [(0, 0, (half,)) for half in both] + [(k, j, both) for k in range(LAST) for j in range(PACK)][1:]
         loads += [(LAST, j, (half,)) for half in both for j in range(PACK)]
         for number, args in enumerate(loads):
             at_step(0 if number < PLANES_AHEAD else 2 * (number - PLANES_AHEAD), 0.5, load, *args)
@@ -288,24 +289,25 @@ def tile_criterionminibatchcrossimagepair_kernel(tc, feat_S, feat_T, out):
                 j, dy = divmod(count, ROW_PAIRS)
                 step = STEPS * k + count
                 if (k, j, dy) in SCALAR_ITEMS:
-                    at_step(step - CONVERT_LEAD, 0.7, convert, k, j, dy)
+                    at_step(step - CONVERT_LEAD, 3.5, convert, k, j, dy)
                     at_step(step, 1, turn_converted, k, j, dy)
                 else:
                     at_step(step, 1, add_rows, k, j, dy, both)
             done = STEPS * k + STEPS - 1
-            at_step(done + NORM_DELAY, 3, norm, k, both)
+            d_norm, d_scale, d_turn, d_quant, d_pairs, rate = DELAYS[k]
+            at_step(done + d_norm, 3, norm, k, both)
             for half in both:
-                at_step(done + SCALE_DELAY, 3, scale_to_unit, k, half)
-            at_step(done + TURN_BACK_DELAY, 3, turn_back, k, both)
+                at_step(done + d_scale, 3, scale_to_unit, k, half)
+            at_step(done + d_turn, 3, turn_back, k, both)
             for half in both:
-                at_step(done + QUANTISE_DELAY, 3, quantise, k, half)
+                at_step(done + d_quant, 3, quantise, k, half)
             if is_teacher(k):
                 at_step(done + NEGATE_DELAY, 3, quantise_negated, k)
             for count, (i, j) in enumerate(new_pairs(k % IMAGES)):
-                step = done + PAIR_DELAY + count
                 if is_teacher(k):
-                    at_step(step, 0, teacher_pair, i, j)
-                else:
+                    at_step(done + d_pairs + count // rate, 0, teacher_pair, i, j)
+                elif k < LAST - 1:
+                    step = done + d_pairs + count // rate
                     blocks = [(i, half, j, slice(0, PIXELS), j) for half in both]
                     at_step(step, 0, student_difs, (i, j), blocks)
                     at_step(step, 0, student_sims, blocks)
@@ -315,70 +317,55 @@ def tile_criterionminibatchcrossimagepair_kernel(tc, feat_S, feat_T, out):
         for half in both:
             for j in range(PACK):
                 for dy in range(ROW_PAIRS):
-                    at_step(STEPS * LAST + half * PACK + j, 1, add_rows, LAST, j, dy, (half,))
+                    step = STEPS * LAST + half * PACK + j
+                    if (LAST, half, j, dy) in LAST_ITEMS:
+                        at_step(step - LAST_LEAD, 2.9, convert, LAST, j, dy, (half,))
+                        at_step(step, 1, turn_converted, LAST, j, dy, (half,))
+                    else:
+                        at_step(step, 1, add_rows, LAST, j, dy, (half,))
         b = LAST % IMAGES
         lo, hi = slice(0, P), slice(P, PIXELS)
         end = POOLING_STEPS
-        before = end - PACK
-        at_step(before, 3, norm, LAST, (0,))
-        at_step(before + 1, 3, scale_to_unit, LAST, 0)
-        at_step(before + 2, 3, turn_back, LAST, (0,))
+        at_step(end - PACK, 3, norm, LAST, (0,))
+        at_step(end - PACK, 3.1, scale_to_unit, LAST, 0)
+        at_step(end - 2, 3, turn_back, LAST, (0,))
         at_step(end - 1, 2.8, quantise, LAST, 0)
         whole = slice(0, PIXELS)
+        two = []
+        for i, j in new_pairs(b - 1):
+            two.append([(i, half, j, whole, j) for half in both])
         early = [
             [(b, 0, 0, whole, 0), (b, 0, 1, whole, 1)],
-            [(b, 0, 2, whole, 2), (b, 0, b, lo, b)],
-            [(0, 0, b, lo, b), (0, 1, b, lo, b), (1, 0, b, lo, b), (1, 1, b, lo, b)],
-            [(2, 0, b, lo, b), (2, 1, b, lo, b)],
+            [(b, 0, 2, whole, 2)],
         ]
         late = [
-            [(b, 1, 0, whole, 0), (b, 1, 1, whole, 1)],
-            [(b, 1, 2, whole, 2), (b, 1, b, whole, b)],
-            [(0, 0, b, hi, IMAGES), (0, 1, b, hi, IMAGES), (1, 0, b, hi, IMAGES), (1, 1, b, hi, IMAGES)],
-            [(2, 0, b, hi, IMAGES), (2, 1, b, hi, IMAGES), (b, 0, b, hi, IMAGES)],
+            [(b, 0, b, whole, b), (b, 1, 0, whole, 0)],
+            [(b, 1, 1, whole, 1), (b, 1, 2, whole, 2)],
+            [(b, 1, b, whole, b), (0, 0, b, whole, b)],
+            [(0, 1, b, whole, b), (1, 0, b, whole, b)],
+            [(1, 1, b, whole, b), (2, 0, b, whole, b)],
+            [(2, 1, b, whole, b)],
         ]
-        pending = [early[0], early[1], early[2], early[3]]
-        seq = [
-            (norm, LAST, (1,)),
-            (student_difs, "e0", early[0], psum_sums), (student_sims, early[0]),
-            (scale_to_unit, LAST, 1),
-            (products, "e0", early[0]),
-            (student_difs, "e1", early[1], psum_turn), (student_sims, early[1]),
-            (turn_back, LAST, (1,)),
-            (products, "e1", early[1]),
-            (quantise, LAST, 1),
-            (student_difs, "e2", early[2], psum_sums), (student_sims, early[2]), (products, "e2", early[2]),
-            (student_difs, "e3", early[3], psum_turn), (student_sims, early[3]), (products, "e3", early[3]),
-            (student_sims, late[0]), (student_difs, "l0", late[0], psum_sums), (products, "l0", late[0]),
-            (student_sims, late[1]), (student_difs, "l1", late[1], psum_sums), (products, "l1", late[1]),
-            (student_sims, late[2]), (student_difs, "l2", late[2], psum_sums), (products, "l2", late[2]),
-            (student_sims, late[3]), (student_difs, "l3", late[3], psum_sums), (products, "l3", late[3]),
-        ]
+        seq = [(norm, LAST, (1,)), (scale_to_unit, LAST, 1), (student_difs, "s0", two[0], psum_sums), (student_difs, "s1", two[1], psum_sums), (products, "s0", two[0]), (student_sims, two[0]), (turn_back, LAST, (1,)), (products, "s1", two[1]), (student_difs, "s2", two[2], psum_turn), (student_sims, two[1]), (products, "s2", two[2]), (quantise, LAST, 1), (student_difs, "s3", two[3], psum_sums), (student_sims, two[2]), (products, "s3", two[3]), (student_difs, "s4", two[4], psum_sums), (student_sims, two[3]), (products, "s4", two[4]), (student_difs, "e0", early[0], psum_sums), (student_sims, two[4]), (products, "e0", early[0]), (student_sims, early[0]), (student_difs, "e1", early[1], psum_sums), (student_sims, early[1]), (products, "e1", early[1]), (student_sims, late[0]), (student_difs, "l0", late[0], psum_sums), (products, "l0", late[0]), (student_sims, late[1]), (student_difs, "l1", late[1], psum_sums), (products, "l1", late[1]), (student_sims, late[2]), (student_difs, "l2", late[2], psum_sums), (products, "l2", late[2]), (student_sims, late[3]), (student_difs, "l3", late[3], psum_sums), (products, "l3", late[3]), (student_sims, late[4]), (student_difs, "l4", late[4], psum_sums), (products, "l4", late[4]), (student_sims, late[5]), (student_difs, "l5", late[5], psum_sums), (products, "l5", late[5])]
         for number, entry in enumerate(seq):
             at_step(end + number, 0, entry[0], *entry[1:])
-        nc.vector.memset(z_s[:], 0.0)
-        nc.vector.memset(cross[:], 0.0)
         ctx.enter_context(tc.manual_schedule())
         for key in sorted(plan):
             for call, args in plan[key]:
                 call(*args)
 
-        nc.vector.tensor_add(out=z_s[:, :, :, b], in0=z_s[:, :, :, b], in1=z_s[:, :, :, IMAGES])
-        nc.vector.tensor_add(out=cross[:, :, :, b], in0=cross[:, :, :, b], in1=cross[:, :, :, IMAGES])
-        ratio = small.tile([P, IMAGES * HALVES, IMAGES], F32)
-        inv_z_rows = inv_z[:].rearrange("p i h j -> p (i h) j")
-        nc.vector.tensor_mul(out=ratio[:], in0=z_s[:].rearrange("p i h j -> p (i h) j")[:, :, 0:IMAGES], in1=inv_z_rows)
-        row_sums = small.tile([P, 2], F32)
-        expected = small.tile([P, IMAGES * HALVES, IMAGES], F32)
-        nc.vector.scalar_tensor_tensor(out=expected[:], in0=cross[:].rearrange("p i h j -> p (i h) j")[:, :, 0:IMAGES], scalar=1.0, in1=inv_z_rows, op0=ALU.mult, op1=ALU.mult, accum_out=row_sums[:, 0:1])
-        log_ratio = small.tile([P, SOFTMAXES], F32)
-        nc.scalar.activation(out=log_ratio[:], in_=ratio[:].rearrange("p r j -> p (r j)"), func=ACT.Ln, accum_out=row_sums[:, 1:2])
+        row_sums = small.tile([P, 3], F32)
+        logs = small.tile([P, SOFTMAXES], F32)
+        nc.scalar.activation(out=logs[:], in_=inv_z[:].rearrange("p i h j -> p (i h j)"), func=ACT.Ln, accum_out=row_sums[:, 1:2])
+        nc.scalar.activation(out=logs[:], in_=z_s[:].rearrange("p i h j -> p (i h j)"), func=ACT.Ln, accum_out=row_sums[:, 2:3])
+        expected = small.tile([P, SOFTMAXES], F32)
+        nc.vector.scalar_tensor_tensor(out=expected[:], in0=cross[:].rearrange("p i h j -> p (i h j)"), scalar=1.0, in1=inv_z[:].rearrange("p i h j -> p (i h j)"), op0=ALU.mult, op1=ALU.mult, accum_out=row_sums[:, 0:1])
         total = psum_turn.tile([P, HALVES * PIXELS], F32, tag="turn", name="total")
-        nc.tensor.matmul(out=total[:, 0:2], lhsT=ones[:], rhs=row_sums[:], start=True, stop=True)
-        scaled = small.tile([P, 2], F32)
+        nc.tensor.matmul(out=total[:, 0:3], lhsT=ones[:], rhs=row_sums[:], start=True, stop=True)
+        scaled = small.tile([P, 3], F32)
         mean = small.tile([P, 1], F32)
         nc.scalar.activation(
-            out=scaled[:], in_=total[:, 0:2], func=ACT.Copy, scale=1.0 / (IMAGES * IMAGES * PIXELS), accum_out=mean[:]
+            out=scaled[:], in_=total[:, 0:3], func=ACT.Copy, scale=1.0 / (IMAGES * IMAGES * PIXELS), accum_out=mean[:]
         )
         out_view = out
         for axis in range(2 - len(out.shape)):

@@ -64,6 +64,8 @@ def tile_criterionminibatchcrossimagepair_kernel(tc, feat_S, feat_T, out):
 
         ident_f32 = const.tile([P, P], F32)
         make_identity(nc, ident_f32[:])
+        ident_bf16 = const.tile([P, P], BF16)
+        make_identity(nc, ident_bf16[:])
         ones = const.tile([P, P], F32)
         nc.vector.memset(ones[:], 1.0)
 
@@ -171,23 +173,24 @@ def tile_criterionminibatchcrossimagepair_kernel(tc, feat_S, feat_T, out):
         def scale_to_unit(k, half):
             unit[k, half] = work.tile([P, CHANNELS], BF16, name="unit")
             nc.scalar.activation(
-                out=unit[k, half][:].rearrange("n (u p e) -> n u p e", u=2, e=2),
-                in_=by_pixel[k, half][:].rearrange("n (u e) p -> n u p e", e=2),
+                out=unit[k, half][:],
+                in_=by_pixel[k, half][:].rearrange("n j p -> n (j p)"),
                 func=ACT.Copy,
                 scale=inv_norm[k, half],
             )
 
         def turn_back(k, halves):
-            back = psum_turn.tile([P, len(halves), 2, P], F32, tag="turn", name="back")
+            back = psum_turn.tile([P, len(halves), PACK, P], BF16, tag="turn", name="back")
             for position, half in enumerate(halves):
-                words = unit[k, half][:].bitcast(F32)
-                for u in range(2):
-                    nc.tensor.transpose(back[:, position, u, :], words[:, u * P : (u + 1) * P], ident_f32[:])
+                for j in range(PACK):
+                    nc.tensor.transpose(
+                        back[:, position, j, :], unit[k, half][:, j * P : (j + 1) * P], ident_bf16[:]
+                    )
             for position, half in enumerate(halves):
                 grouped[k, half] = kept.tile([P, P * PACK], BF16, name="grouped", align_bytes=64)
                 nc.scalar.copy(
-                    out=grouped[k, half][:].bitcast(F32).rearrange("p (n u) -> p n u", u=2),
-                    in_=back[:, position].rearrange("p u n -> p n u"),
+                    out=grouped[k, half][:].rearrange("p (n j) -> p n j", j=PACK),
+                    in_=back[:, position].rearrange("p j n -> p n j"),
                 )
 
         def quantise_as(name, b, half, values):

@@ -23,7 +23,7 @@ PIXELS = GRID * GRID
 PACK = CHANNELS // P
 HALVES = PIXELS // P
 HALF_PLANE = SIDE * SIDE // HALVES
-ROWS = IMAGES * PIXELS
+BOTH = (0, 1)
 SOFTMAXES = IMAGES * HALVES * IMAGES
 INV_TEMPERATURE = 10.0
 NORM_FLOOR_SQUARED = (PATCH * PATCH * 1e-12) ** 2
@@ -31,15 +31,23 @@ NORM_FLOOR_SQUARED = (PATCH * PATCH * 1e-12) ** 2
 ROW_PAIRS = PATCH // 2
 STEPS = PACK * ROW_PAIRS
 POOLING_STEPS = STEPS * ALL_IMAGES
-PLANES_AHEAD = 10
-SCALAR_ITEMS = ()
-CONVERT_LEAD = 4
-LAST_LEAD = 2
-LAST_ITEMS = ()
-DELAYS = [(1,2,6,9,10,1)]*5+[(1,1,4,8,9,2),(2,2,4,7,0,1)]
+PLANES_AHEAD = 8
+CONVERTED = ((1, 1), (2, 1))
+CONVERT_LEAD = 5
 
-NEGATE_DELAY = 11
-PRODUCT_LAG = 1
+TEACHER_NORM_DELAY = 2
+STUDENT_NORM_DELAY = 1
+TURN_BACK_DELAY = 6
+TEACHER_QUANTISE_DELAY = 12
+STUDENT_QUANTISE_DELAY = 8
+LAST_TURN_BACK_DELAY = 3
+LAST_QUANTISE_DELAY = 4
+PRODUCT_DELAY = 2
+TEACHER_PAIRS_A_STEP = 2
+DEFERRED_FROM = 1
+LAST_TURN_AT = 4
+
+PAIRS, LOADS, SUMS, PRODUCTS, STAGES, CONVERSIONS = range(6)
 
 FLOPS = 2 * IMAGES * IMAGES * 2 * PIXELS * PIXELS * CHANNELS
 
@@ -48,17 +56,20 @@ def new_pairs(b):
     return [(b, j) for j in range(b + 1)] + [(i, b) for i in range(b)]
 
 
+def row_blocks(i, j):
+    return tuple((i, half, j) for half in BOTH)
+
+
 def tile_criterionminibatchcrossimagepair_kernel(tc, feat_S, feat_T, out):
     nc = tc.nc
     with ExitStack() as ctx:
         const = ctx.enter_context(tc.tile_pool(name="const", bufs=1))
-        raw_pool = ctx.enter_context(tc.tile_pool(name="raw", bufs=PLANES_AHEAD + 1))
-        partial_pool = ctx.enter_context(tc.tile_pool(name="partial", bufs=8))
+        raw_pool = ctx.enter_context(tc.tile_pool(name="raw", bufs=PLANES_AHEAD + PACK))
+        partial_pool = ctx.enter_context(tc.tile_pool(name="partial", bufs=6))
         converted_pool = ctx.enter_context(tc.tile_pool(name="converted", bufs=4))
-        small = ctx.enter_context(tc.tile_pool(name="small", bufs=6))
+        small = ctx.enter_context(tc.tile_pool(name="small", bufs=4))
         work = ctx.enter_context(tc.tile_pool(name="work", bufs=4))
-        kept = ctx.enter_context(tc.tile_pool(name="kept", bufs=4))
-        unread = ctx.enter_context(tc.tile_pool(name="unread", bufs=4))
+        unread = ctx.enter_context(tc.tile_pool(name="unread", bufs=2))
         psum_sums = ctx.enter_context(tc.psum_pool(name="psum_sums", bufs=2 * HALVES))
         psum_turn = ctx.enter_context(tc.psum_pool(name="psum_turn", bufs=4))
 
@@ -69,16 +80,14 @@ def tile_criterionminibatchcrossimagepair_kernel(tc, feat_S, feat_T, out):
         ones = const.tile([P, P], F32)
         nc.vector.memset(ones[:], 1.0)
 
-        operands = {}
-        for name in ("T", "minus_T", "S"):
-            codes = const.tile([P, ROWS], U32, name="codes_" + name, align_bytes=64)
-            scales = const.tile([P, ROWS], U8, name="scales_" + name, align_bytes=64)
-            operands[name] = {"codes": codes, "scales": scales}
+        codes_T = const.tile([P, IMAGES, 2, PIXELS], U32, align_bytes=64)
+        scales_T = const.tile([P, IMAGES, 2, PIXELS], U8, align_bytes=64)
+        codes_S = const.tile([P, IMAGES, PIXELS], U32, align_bytes=64)
+        scales_S = const.tile([P, IMAGES, PIXELS], U8, align_bytes=64)
         z_t = const.tile([P, IMAGES, HALVES, IMAGES], F32)
         inv_z = const.tile([P, IMAGES, HALVES, IMAGES], F32)
         z_s = const.tile([P, IMAGES, HALVES, IMAGES], F32)
         cross = const.tile([P, IMAGES, HALVES, IMAGES], F32)
-
         exp_t = const.tile([P, IMAGES, IMAGES, HALVES, PIXELS], F32)
 
         raw = {}
@@ -92,63 +101,61 @@ def tile_criterionminibatchcrossimagepair_kernel(tc, feat_S, feat_T, out):
         def is_teacher(k):
             return k < IMAGES
 
+
         def load(k, j, halves):
             feat = feat_T if is_teacher(k) else feat_S
-            plane = feat[k % IMAGES].rearrange("(p j) h w -> p j (h w)", j=PACK)[:, j, :]
+            planes = feat[k % IMAGES].rearrange("(p j) h w -> p j (h w)", j=PACK)
             if halves[0] == 0:
                 raw[k, j] = raw_pool.tile([P, SIDE * SIDE], BF16, name="raw")
             span = slice(halves[0] * HALF_PLANE, (halves[-1] + 1) * HALF_PLANE)
-            nc.sync.dma_start(out=raw[k, j][:, span], in_=plane[:, span])
+            nc.sync.dma_start(out=raw[k, j][:, span], in_=planes[:, j, span])
 
         def places(k, j, halves):
             span = slice(halves[0] * HALF_PLANE, (halves[-1] + 1) * HALF_PLANE)
-            return raw[k, j][:, span].rearrange(
-                "p (y dy x dx) -> p dy dx y x", dy=PATCH, x=GRID, dx=PATCH
-            )
+            return raw[k, j][:, span].rearrange("p (y dy x dx) -> p dy dx y x", dy=PATCH, x=GRID, dx=PATCH)
 
-        def turn(k, j, halves, partial, first, last):
-            for position, half in enumerate(halves):
-                if j == 0 and first:
-                    by_pixel[k, half] = psum_sums.tile([P, PACK, P], F32, tag="sums", name="by_pixel")
-                for dx in range(PATCH):
-                    nc.tensor.matmul(
-                        out=by_pixel[k, half][:, j, :],
-                        lhsT=partial[:, dx, position * P : (position + 1) * P],
-                        rhs=ident_f32[:],
-                        is_transpose=True,
-                        start=(first and dx == 0),
-                        stop=(last and dx == PATCH - 1),
-                    )
+        def turn(k, j, half, source, first, last):
+            for dx in range(PATCH):
+                nc.tensor.matmul(
+                    out=by_pixel[k, half][:, j, :],
+                    lhsT=source[:, dx, :],
+                    rhs=ident_f32[:],
+                    is_transpose=True,
+                    start=(first and dx == 0),
+                    stop=(last and dx == PATCH - 1),
+                )
 
-        def add_rows(k, j, dy, halves):
-            partial = partial_pool.tile([P, PATCH, len(halves) * P], F32, name="partial")
-            parts = [(half,) for half in halves] if k == 0 and j == 0 else [halves]
-            for part in parts:
-                source = places(k, j, part)
-                at = (part[0] - halves[0]) * P
+        def add_rows(k, j, dy, halves, pieces):
+            width = len(halves) * P
+            sums = partial_pool.tile([P, PATCH, width], F32, name="sums_%d" % width)
+            for piece in pieces:
+                source = places(k, j, piece)
+                at = (piece[0] - halves[0]) * P
                 nc.vector.tensor_tensor(
-                    out=partial[:, :, at : at + len(part) * P].rearrange("p dx (y x) -> p dx y x", x=GRID),
+                    out=sums[:, :, at : at + len(piece) * P].rearrange("p dx (y x) -> p dx y x", x=GRID),
                     in0=source[:, dy],
                     in1=source[:, dy + ROW_PAIRS],
                     op=ALU.add,
                 )
-            turn(k, j, halves, partial, dy == 0, dy == ROW_PAIRS - 1)
+            for position, half in enumerate(halves):
+                if j == 0 and dy == 0:
+                    by_pixel[k, half] = psum_sums.tile([P, PACK, P], F32, tag="sums", name="by_pixel")
+                turn(k, j, half, sums[:, :, position * P : (position + 1) * P], dy == 0, dy == ROW_PAIRS - 1)
 
-        def convert(k, j, dy, halves=(0, 1)):
-            converted[k, j, dy, halves] = []
-            for row in (dy, dy + ROW_PAIRS):
-                tile = converted_pool.tile([P, PATCH, len(halves) * P], F32, name="converted")
-                nc.scalar.copy(
-                    out=tile[:].rearrange("p dx (y x) -> p dx y x", x=GRID),
-                    in_=places(k, j, halves)[:, row],
-                )
-                converted[k, j, dy, halves].append(tile)
+        def convert_row(k, j, row):
+            converted[k, j, row] = converted_pool.tile([P, PATCH, PIXELS], F32, name="converted")
+            nc.scalar.copy(
+                out=converted[k, j, row][:].rearrange("p dx (y x) -> p dx y x", x=GRID),
+                in_=places(k, j, BOTH)[:, row],
+            )
 
-        def turn_converted(k, j, dy, halves=(0, 1)):
-            for number, tile in enumerate(converted[k, j, dy, halves]):
-                turn(k, j, halves, tile, dy == 0 and number == 0, dy == ROW_PAIRS - 1 and number == 1)
+        def turn_converted(k, j, rows):
+            for half in BOTH:
+                for row in rows:
+                    turn(k, j, half, converted[k, j, row][:, :, half * P : (half + 1) * P], False, row == rows[-1])
 
-        def norm(k, halves):
+
+        def norm_and_scale(k, halves):
             square_sum = small.tile([P, HALVES], F32)
             for half in halves:
                 squares = unread.tile([P, CHANNELS], F32)
@@ -168,16 +175,13 @@ def tile_criterionminibatchcrossimagepair_kernel(tc, feat_S, feat_T, out):
                 out=inverse[:, span], in_=above_floor[:, span], func=ACT.Abs_reciprocal_sqrt, bias=NORM_FLOOR_SQUARED
             )
             for half in halves:
-                inv_norm[k, half] = inverse[:, half : half + 1]
-
-        def scale_to_unit(k, half):
-            unit[k, half] = work.tile([P, CHANNELS], BF16, name="unit")
-            nc.scalar.activation(
-                out=unit[k, half][:],
-                in_=by_pixel[k, half][:].rearrange("n j p -> n (j p)"),
-                func=ACT.Copy,
-                scale=inv_norm[k, half],
-            )
+                unit[k, half] = work.tile([P, CHANNELS], BF16, name="unit")
+                nc.scalar.activation(
+                    out=unit[k, half][:],
+                    in_=by_pixel[k, half][:].rearrange("n j p -> n (j p)"),
+                    func=ACT.Copy,
+                    scale=inverse[:, half : half + 1],
+                )
 
         def turn_back(k, halves):
             back = psum_turn.tile([P, len(halves), PACK, P], BF16, tag="turn", name="back")
@@ -186,189 +190,197 @@ def tile_criterionminibatchcrossimagepair_kernel(tc, feat_S, feat_T, out):
                     nc.tensor.transpose(
                         back[:, position, j, :], unit[k, half][:, j * P : (j + 1) * P], ident_bf16[:]
                     )
-            for position, half in enumerate(halves):
-                grouped[k, half] = kept.tile([P, P * PACK], BF16, name="grouped", align_bytes=64)
-                nc.scalar.copy(
-                    out=grouped[k, half][:].rearrange("p (n j) -> p n j", j=PACK),
-                    in_=back[:, position].rearrange("p j n -> p n j"),
-                )
-
-        def quantise_as(name, b, half, values):
-            cols = slice(b * PIXELS + half * P, b * PIXELS + (half + 1) * P)
-            nc.vector.quantize_mx(
-                out=operands[name]["codes"][:, cols].bitcast(FP8X4),
-                scales=operands[name]["scales"][:, cols],
-                in_=values[:],
+            if halves[0] == 0:
+                signs = 2 if is_teacher(k) else 1
+                grouped[k] = work.tile([P, signs, PIXELS * PACK], BF16, name="grouped_%d" % signs, align_bytes=64)
+            span = slice(halves[0] * P * PACK, (halves[-1] + 1) * P * PACK)
+            nc.scalar.copy(
+                out=grouped[k][:, 0, span].rearrange("p (h n j) -> p h n j", h=len(halves), j=PACK),
+                in_=back[:].rearrange("p h j n -> p h n j"),
             )
 
-        def quantise(k, half):
-            quantise_as("T" if is_teacher(k) else "S", k % IMAGES, half, grouped[k, half])
+        def quantise(k, halves):
+            b = k % IMAGES
+            if is_teacher(k):
+                nc.vector.tensor_scalar_mul(out=grouped[k][:, 1, :], in0=grouped[k][:, 0, :], scalar1=-1.0)
+                nc.vector.quantize_mx(
+                    out=codes_T[:, b].rearrange("p s n -> p (s n)").bitcast(FP8X4),
+                    scales=scales_T[:, b].rearrange("p s n -> p (s n)"),
+                    in_=grouped[k][:].rearrange("p s m -> p (s m)"),
+                )
+            else:
+                span = slice(halves[0] * P, (halves[-1] + 1) * P)
+                nc.vector.quantize_mx(
+                    out=codes_S[:, b, span].bitcast(FP8X4),
+                    scales=scales_S[:, b, span],
+                    in_=grouped[k][:, 0, span.start * PACK : span.stop * PACK],
+                )
 
-        def quantise_negated(k):
-            negated = {}
-            for half in range(HALVES):
-                negated[half] = work.tile([P, P * PACK], BF16, name="negated", align_bytes=64)
-                nc.vector.tensor_scalar_mul(out=negated[half][:], in0=grouped[k, half][:], scalar1=-1.0)
-            for half in range(HALVES):
-                quantise_as("minus_T", k, half, negated[half])
 
-        def similarity(acc, passes, i, half, j, cols):
-            rows = slice(i * PIXELS + half * P, i * PIXELS + (half + 1) * P)
-            span = slice(j * PIXELS + cols.start, j * PIXELS + cols.stop)
+        def operand(name, b, span):
+            if name == "S":
+                return codes_S[:, b, span].bitcast(FP8X4), scales_S[:, b, span]
+            sign = 1 if name == "minus_T" else 0
+            return codes_T[:, b, sign, span].bitcast(FP8X4), scales_T[:, b, sign, span]
+
+        def similarity(acc, passes, i, half, j):
             for number, (left, right) in enumerate(passes):
+                lhs, lhs_scale = operand(left, i, slice(half * P, (half + 1) * P))
+                rhs, rhs_scale = operand(right, j, slice(0, PIXELS))
                 nc.tensor.matmul_mx(
                     out=acc,
-                    lhsT=operands[left]["codes"][:, rows].bitcast(FP8X4),
-                    lhsT_scale=operands[left]["scales"][:, rows],
-                    rhs=operands[right]["codes"][:, span].bitcast(FP8X4),
-                    rhs_scale=operands[right]["scales"][:, span],
+                    lhsT=lhs,
+                    lhsT_scale=lhs_scale,
+                    rhs=rhs,
+                    rhs_scale=rhs_scale,
                     start=(number == 0),
                     stop=(number == len(passes) - 1),
                 )
 
         def shifted_exp(result, sim, row_sum):
             nc.scalar.activation(
-                out=result, in_=sim, func=ACT.Exp, scale=INV_TEMPERATURE, bias=-INV_TEMPERATURE,
-                accum_out=row_sum,
+                out=result, in_=sim, func=ACT.Exp, scale=INV_TEMPERATURE, bias=-INV_TEMPERATURE, accum_out=row_sum
             )
 
-        def teacher_pair(i, j):
+        def teacher_sims(blocks):
             sim = psum_turn.tile([P, HALVES, PIXELS], F32, tag="turn", name="sim_t")
-            for half in range(HALVES):
-                similarity(sim[:, half, :], (("T", "T"),), i, half, j, slice(0, PIXELS))
-            for half in range(HALVES):
-                shifted_exp(exp_t[:, i, j, half, :], sim[:, half, :], z_t[:, i, half, j : j + 1])
+            for number, (i, half, j) in enumerate(blocks):
+                similarity(sim[:, number, :], (("T", "T"),), i, half, j)
+            for number, (i, half, j) in enumerate(blocks):
+                shifted_exp(exp_t[:, i, j, half, :], sim[:, number, :], z_t[:, i, half, j : j + 1])
 
         def student_sims(blocks):
-            sim = psum_turn.tile([P, HALVES * PIXELS], F32, tag="turn", name="sim_s")
-            at = 0
-            spans = []
-            for i, half, j, cols, slot in blocks:
-                width = cols.stop - cols.start
-                spans.append(slice(at, at + width))
-                at += width
-            for (i, half, j, cols, slot), span in zip(blocks, spans):
-                similarity(sim[:, span], (("S", "S"),), i, half, j, cols)
-            for (i, half, j, cols, slot), span in zip(blocks, spans):
+            sim = psum_turn.tile([P, HALVES, PIXELS], F32, tag="turn", name="sim_s")
+            for number, (i, half, j) in enumerate(blocks):
+                similarity(sim[:, number, :], (("S", "S"),), i, half, j)
+            for number, (i, half, j) in enumerate(blocks):
                 exp_s = unread.tile([P, PIXELS], F32)
-                shifted_exp(exp_s[:, 0 : cols.stop - cols.start], sim[:, span], z_s[:, i, half, slot : slot + 1])
+                shifted_exp(exp_s[:], sim[:, number, :], z_s[:, i, half, j : j + 1])
 
-        def student_difs(key, blocks, pool=psum_turn):
-            dif[key] = pool.tile([P, HALVES * PIXELS], F32, tag="sums" if pool is psum_sums else "turn", name="dif")
-            at = 0
-            for i, half, j, cols, slot in blocks:
-                width = cols.stop - cols.start
-                similarity(dif[key][:, at : at + width], (("S", "S"), ("T", "minus_T")), i, half, j, cols)
-                at += width
+        def differences(blocks, pool, tag):
+            dif[blocks] = pool.tile([P, HALVES, PIXELS], F32, tag=tag, name="dif")
+            for number, (i, half, j) in enumerate(blocks):
+                similarity(dif[blocks][:, number, :], (("S", "S"), ("T", "minus_T")), i, half, j)
 
-        def products(key, blocks):
-            at = 0
-            for i, half, j, cols, slot in blocks:
-                width = cols.stop - cols.start
+        def products(blocks):
+            for number, (i, half, j) in enumerate(blocks):
                 weighted = unread.tile([P, PIXELS], F32)
                 nc.vector.scalar_tensor_tensor(
-                    out=weighted[:, 0:width],
-                    in0=dif[key][:, at : at + width],
+                    out=weighted[:],
+                    in0=dif[blocks][:, number, :],
                     scalar=-INV_TEMPERATURE,
-                    in1=exp_t[:, i, j, half, cols],
+                    in1=exp_t[:, i, j, half, :],
                     op0=ALU.mult,
                     op1=ALU.mult,
-                    accum_out=cross[:, i, half, slot : slot + 1],
+                    accum_out=cross[:, i, half, j : j + 1],
                 )
-                at += width
+
+        def flat(columns):
+            return columns[:].rearrange("p i h j -> p (i h j)")
+
 
         plan = {}
 
-        def at_step(step, rank, call, *args):
-            plan.setdefault((step, rank), []).append((call, args))
+        def at_step(step, kind, call, *args):
+            plan.setdefault((max(0, step), kind), []).append((call, args))
 
-        both = (0, 1)
-        loads = [(0, 0, (half,)) for half in both] + [(k, j, both) for k in range(LAST) for j in range(PACK)][1:]
-        loads += [(LAST, j, (half,)) for half in both for j in range(PACK)]
-        for number, args in enumerate(loads):
-            at_step(0 if number < PLANES_AHEAD else 2 * (number - PLANES_AHEAD), 0.5, load, *args)
         for k in range(LAST):
-            for count in range(STEPS):
-                j, dy = divmod(count, ROW_PAIRS)
-                step = STEPS * k + count
-                if (k, j, dy) in SCALAR_ITEMS:
-                    at_step(step - CONVERT_LEAD, 3.5, convert, k, j, dy)
-                    at_step(step, 1, turn_converted, k, j, dy)
-                else:
-                    at_step(step, 1, add_rows, k, j, dy, both)
-            done = STEPS * k + STEPS - 1
-            d_norm, d_scale, d_turn, d_quant, d_pairs, rate = DELAYS[k]
-            at_step(done + d_norm, 3, norm, k, both)
-            for half in both:
-                at_step(done + d_scale, 3, scale_to_unit, k, half)
-            at_step(done + d_turn, 3, turn_back, k, both)
-            for half in both:
-                at_step(done + d_quant, 3, quantise, k, half)
-            if is_teacher(k):
-                at_step(done + NEGATE_DELAY, 3, quantise_negated, k)
-            for count, (i, j) in enumerate(new_pairs(k % IMAGES)):
-                if is_teacher(k):
-                    at_step(done + d_pairs + count // rate, 0, teacher_pair, i, j)
-                elif k < LAST - 1:
-                    step = done + d_pairs + count // rate
-                    blocks = [(i, half, j, slice(0, PIXELS), j) for half in both]
-                    at_step(step, 0, student_difs, (i, j), blocks)
-                    at_step(step, 0, student_sims, blocks)
-                    at_step(step + PRODUCT_LAG, 2, products, (i, j), blocks)
-        at_step(POOLING_STEPS - 2, 2.5, nc.vector.reciprocal, inv_z[:].rearrange("p i h j -> p (i h j)"), z_t[:].rearrange("p i h j -> p (i h j)"))
-
-        for half in both:
             for j in range(PACK):
+                step = STEPS * k + ROW_PAIRS * j
+                pieces = [(0,), (1,)] if (k, j) == (0, 0) else [BOTH]
+                for piece in pieces:
+                    at_step(step - ROW_PAIRS * PLANES_AHEAD, LOADS, load, k, j, piece)
+                at_step(step, SUMS, add_rows, k, j, 0, BOTH, pieces)
+                if (k, j) in CONVERTED:
+                    rows = (1, 1 + ROW_PAIRS)
+                    for number, row in enumerate(rows):
+                        at_step(step - CONVERT_LEAD + 2 * number, CONVERSIONS, convert_row, k, j, row)
+                    at_step(step + 1, SUMS, turn_converted, k, j, rows)
+                else:
+                    at_step(step + 1, SUMS, add_rows, k, j, 1, BOTH, pieces)
+        for half in BOTH:
+            for j in range(PACK):
+                step = STEPS * LAST + PACK * half + j
+                at_step(step - ROW_PAIRS * PLANES_AHEAD, LOADS, load, LAST, j, (half,))
                 for dy in range(ROW_PAIRS):
-                    step = STEPS * LAST + half * PACK + j
-                    if (LAST, half, j, dy) in LAST_ITEMS:
-                        at_step(step - LAST_LEAD, 2.9, convert, LAST, j, dy, (half,))
-                        at_step(step, 1, turn_converted, LAST, j, dy, (half,))
-                    else:
-                        at_step(step, 1, add_rows, LAST, j, dy, (half,))
-        b = LAST % IMAGES
-        lo, hi = slice(0, P), slice(P, PIXELS)
-        end = POOLING_STEPS
-        at_step(end - PACK, 3, norm, LAST, (0,))
-        at_step(end - PACK, 3.1, scale_to_unit, LAST, 0)
-        at_step(end - 2, 3, turn_back, LAST, (0,))
-        at_step(end - 1, 2.8, quantise, LAST, 0)
-        whole = slice(0, PIXELS)
-        two = []
-        for i, j in new_pairs(b - 1):
-            two.append([(i, half, j, whole, j) for half in both])
-        early = [
-            [(b, 0, 0, whole, 0), (b, 0, 1, whole, 1)],
-            [(b, 0, 2, whole, 2)],
-        ]
-        late = [
-            [(b, 0, b, whole, b), (b, 1, 0, whole, 0)],
-            [(b, 1, 1, whole, 1), (b, 1, 2, whole, 2)],
-            [(b, 1, b, whole, b), (0, 0, b, whole, b)],
-            [(0, 1, b, whole, b), (1, 0, b, whole, b)],
-            [(1, 1, b, whole, b), (2, 0, b, whole, b)],
-            [(2, 1, b, whole, b)],
-        ]
-        seq = [(norm, LAST, (1,)), (scale_to_unit, LAST, 1), (student_difs, "s0", two[0], psum_sums), (student_difs, "s1", two[1], psum_sums), (products, "s0", two[0]), (student_sims, two[0]), (turn_back, LAST, (1,)), (products, "s1", two[1]), (student_difs, "s2", two[2], psum_turn), (student_sims, two[1]), (products, "s2", two[2]), (quantise, LAST, 1), (student_difs, "s3", two[3], psum_sums), (student_sims, two[2]), (products, "s3", two[3]), (student_difs, "s4", two[4], psum_sums), (student_sims, two[3]), (products, "s4", two[4]), (student_difs, "e0", early[0], psum_sums), (student_sims, two[4]), (products, "e0", early[0]), (student_sims, early[0]), (student_difs, "e1", early[1], psum_sums), (student_sims, early[1]), (products, "e1", early[1]), (student_sims, late[0]), (student_difs, "l0", late[0], psum_sums), (products, "l0", late[0]), (student_sims, late[1]), (student_difs, "l1", late[1], psum_sums), (products, "l1", late[1]), (student_sims, late[2]), (student_difs, "l2", late[2], psum_sums), (products, "l2", late[2]), (student_sims, late[3]), (student_difs, "l3", late[3], psum_sums), (products, "l3", late[3]), (student_sims, late[4]), (student_difs, "l4", late[4], psum_sums), (products, "l4", late[4]), (student_sims, late[5]), (student_difs, "l5", late[5], psum_sums), (products, "l5", late[5])]
-        for number, entry in enumerate(seq):
-            at_step(end + number, 0, entry[0], *entry[1:])
+                    at_step(step, SUMS, add_rows, LAST, j, dy, (half,), [(half,)])
+
+        for k in range(LAST):
+            b = k % IMAGES
+            done = STEPS * k + STEPS - 1
+            quantised = done + (TEACHER_QUANTISE_DELAY if is_teacher(k) else STUDENT_QUANTISE_DELAY)
+            if k == IMAGES:
+                quantised += 1
+            norm_delay = TEACHER_NORM_DELAY if is_teacher(k) else STUDENT_NORM_DELAY
+            at_step(done + norm_delay, STAGES, norm_and_scale, k, BOTH)
+            at_step(done + TURN_BACK_DELAY, STAGES, turn_back, k, BOTH)
+            at_step(quantised, STAGES, quantise, k, BOTH)
+            for number, (i, j) in enumerate(new_pairs(b)):
+                blocks = row_blocks(i, j)
+                if is_teacher(k):
+                    at_step(quantised + 1 + number // TEACHER_PAIRS_A_STEP, PAIRS, teacher_sims, blocks)
+                elif k < LAST - 1:
+                    at_step(quantised + 1, PAIRS, student_sims, blocks)
+                    if b < DEFERRED_FROM:
+                        at_step(quantised + 1, PAIRS, differences, blocks, psum_turn, "turn")
+                        at_step(quantised + 1 + PRODUCT_DELAY, PRODUCTS, products, blocks)
+        done = POOLING_STEPS - PACK - 1
+        at_step(done + STUDENT_NORM_DELAY, STAGES, norm_and_scale, LAST, (0,))
+        at_step(done + LAST_TURN_BACK_DELAY, STAGES, turn_back, LAST, (0,))
+        at_step(done + LAST_QUANTISE_DELAY, STAGES, quantise, LAST, (0,))
+        at_step(done + LAST_TURN_BACK_DELAY, STAGES, nc.vector.reciprocal, flat(inv_z), flat(z_t))
+
         ctx.enter_context(tc.manual_schedule())
         for key in sorted(plan):
             for call, args in plan[key]:
                 call(*args)
 
+        b = LAST % IMAGES
+        without_last = [row_blocks(i, j) for image in range(DEFERRED_FROM, b) for i, j in new_pairs(image)]
+        exps_done = len(new_pairs(DEFERRED_FROM))
+        first_half = [(b, 0, j) for j in range(b)]
+        second_half = [(b, 0, b)] + [(b, 1, j) for j in range(b + 1)] + [(i, half, b) for i in range(b) for half in BOTH]
+        groups = without_last
+        for blocks in (first_half, second_half):
+            groups = groups + [tuple(blocks[at : at + HALVES]) for at in range(0, len(blocks), HALVES)]
+
+        norm_and_scale(LAST, (1,))
+        for number in range(len(groups) + 2):
+            if number == LAST_TURN_AT:
+                turn_back(LAST, (1,))
+            if number == LAST_TURN_AT + 1:
+                quantise(LAST, (1,))
+            if number >= 2:
+                products(groups[number - 2])
+            if exps_done < number <= len(groups):
+                student_sims(groups[number - 1])
+            if number < len(groups):
+                differences(groups[number], psum_sums, "sums")
+
         row_sums = small.tile([P, 3], F32)
         logs = small.tile([P, SOFTMAXES], F32)
-        nc.scalar.activation(out=logs[:], in_=inv_z[:].rearrange("p i h j -> p (i h j)"), func=ACT.Ln, accum_out=row_sums[:, 1:2])
-        nc.scalar.activation(out=logs[:], in_=z_s[:].rearrange("p i h j -> p (i h j)"), func=ACT.Ln, accum_out=row_sums[:, 2:3])
+        nc.scalar.activation(out=logs[:], in_=flat(inv_z), func=ACT.Ln, accum_out=row_sums[:, 1:2])
+        nc.scalar.activation(out=logs[:], in_=flat(z_s), func=ACT.Ln, accum_out=row_sums[:, 2:3])
         expected = small.tile([P, SOFTMAXES], F32)
-        nc.vector.scalar_tensor_tensor(out=expected[:], in0=cross[:].rearrange("p i h j -> p (i h j)"), scalar=1.0, in1=inv_z[:].rearrange("p i h j -> p (i h j)"), op0=ALU.mult, op1=ALU.mult, accum_out=row_sums[:, 0:1])
-        total = psum_turn.tile([P, HALVES * PIXELS], F32, tag="turn", name="total")
-        nc.tensor.matmul(out=total[:, 0:3], lhsT=ones[:], rhs=row_sums[:], start=True, stop=True)
+        nc.vector.scalar_tensor_tensor(
+            out=expected[:],
+            in0=flat(cross),
+            scalar=1.0,
+            in1=flat(inv_z),
+            op0=ALU.mult,
+            op1=ALU.mult,
+            accum_out=row_sums[:, 0:1],
+        )
+        total = psum_turn.tile([P, HALVES, PIXELS], F32, tag="turn", name="total")
+        nc.tensor.matmul(out=total[:, 0, 0:3], lhsT=ones[:], rhs=row_sums[:], start=True, stop=True)
         scaled = small.tile([P, 3], F32)
         mean = small.tile([P, 1], F32)
         nc.scalar.activation(
-            out=scaled[:], in_=total[:, 0:3], func=ACT.Copy, scale=1.0 / (IMAGES * IMAGES * PIXELS), accum_out=mean[:]
+            out=scaled[:],
+            in_=total[:, 0, 0:3],
+            func=ACT.Copy,
+            scale=1.0 / (IMAGES * IMAGES * PIXELS),
+            accum_out=mean[:],
         )
         out_view = out
         for axis in range(2 - len(out.shape)):

from contextlib import ExitStack

import concourse.mybir as mybir
from concourse.masks import make_identity

F32 = mybir.dt.float32
BF16 = mybir.dt.bfloat16
U32 = mybir.dt.uint32
U8 = mybir.dt.uint8
FP8X4 = mybir.dt.float8_e4m3fn_x4
ACT = mybir.ActivationFunctionType
ALU = mybir.AluOpType

P = 128
IMAGES = 4
ALL_IMAGES = 2 * IMAGES
LAST = ALL_IMAGES - 1
CHANNELS = 512
SIDE = 64
PATCH = 4
GRID = SIDE // PATCH
PIXELS = GRID * GRID
PACK = CHANNELS // P
HALVES = PIXELS // P
HALF_PLANE = SIDE * SIDE // HALVES
BOTH = (0, 1)
SOFTMAXES = IMAGES * HALVES * IMAGES
INV_TEMPERATURE = 10.0
NORM_FLOOR_SQUARED = (PATCH * PATCH * 1e-12) ** 2

ROW_PAIRS = PATCH // 2
STEPS = PACK * ROW_PAIRS
POOLING_STEPS = STEPS * ALL_IMAGES
PLANES_AHEAD = 8
CONVERTED = ((1, 1), (2, 1))
CONVERT_LEAD = 5

TEACHER_NORM_DELAY = 2
STUDENT_NORM_DELAY = 1
TURN_BACK_DELAY = 6
TEACHER_QUANTISE_DELAY = 12
STUDENT_QUANTISE_DELAY = 8
LAST_TURN_BACK_DELAY = 3
LAST_QUANTISE_DELAY = 4
PRODUCT_DELAY = 2
TEACHER_PAIRS_A_STEP = 2
DEFERRED_FROM = 1
LAST_TURN_AT = 4

PAIRS, LOADS, SUMS, PRODUCTS, STAGES, CONVERSIONS = range(6)

FLOPS = 2 * IMAGES * IMAGES * 2 * PIXELS * PIXELS * CHANNELS


def new_pairs(b):
    return [(b, j) for j in range(b + 1)] + [(i, b) for i in range(b)]


def row_blocks(i, j):
    return tuple((i, half, j) for half in BOTH)


def tile_criterionminibatchcrossimagepair_kernel(tc, feat_S, feat_T, out):
    nc = tc.nc
    with ExitStack() as ctx:
        const = ctx.enter_context(tc.tile_pool(name="const", bufs=1))
        raw_pool = ctx.enter_context(tc.tile_pool(name="raw", bufs=PLANES_AHEAD + PACK))
        partial_pool = ctx.enter_context(tc.tile_pool(name="partial", bufs=6))
        converted_pool = ctx.enter_context(tc.tile_pool(name="converted", bufs=4))
        small = ctx.enter_context(tc.tile_pool(name="small", bufs=4))
        work = ctx.enter_context(tc.tile_pool(name="work", bufs=4))
        unread = ctx.enter_context(tc.tile_pool(name="unread", bufs=2))
        psum_sums = ctx.enter_context(tc.psum_pool(name="psum_sums", bufs=2 * HALVES))
        psum_turn = ctx.enter_context(tc.psum_pool(name="psum_turn", bufs=4))

        ident_f32 = const.tile([P, P], F32)
        make_identity(nc, ident_f32[:])
        ident_bf16 = const.tile([P, P], BF16)
        make_identity(nc, ident_bf16[:])
        ones = const.tile([P, P], F32)
        nc.vector.memset(ones[:], 1.0)

        codes_T = const.tile([P, IMAGES, 2, PIXELS], U32, align_bytes=64)
        scales_T = const.tile([P, IMAGES, 2, PIXELS], U8, align_bytes=64)
        codes_S = const.tile([P, IMAGES, PIXELS], U32, align_bytes=64)
        scales_S = const.tile([P, IMAGES, PIXELS], U8, align_bytes=64)
        z_t = const.tile([P, IMAGES, HALVES, IMAGES], F32)
        inv_z = const.tile([P, IMAGES, HALVES, IMAGES], F32)
        z_s = const.tile([P, IMAGES, HALVES, IMAGES], F32)
        cross = const.tile([P, IMAGES, HALVES, IMAGES], F32)
        exp_t = const.tile([P, IMAGES, IMAGES, HALVES, PIXELS], F32)

        raw = {}
        converted = {}
        by_pixel = {}
        inv_norm = {}
        unit = {}
        grouped = {}
        dif = {}

        def is_teacher(k):
            return k < IMAGES


        def load(k, j, halves):
            feat = feat_T if is_teacher(k) else feat_S
            planes = feat[k % IMAGES].rearrange("(p j) h w -> p j (h w)", j=PACK)
            if halves[0] == 0:
                raw[k, j] = raw_pool.tile([P, SIDE * SIDE], BF16, name="raw")
            span = slice(halves[0] * HALF_PLANE, (halves[-1] + 1) * HALF_PLANE)
            nc.sync.dma_start(out=raw[k, j][:, span], in_=planes[:, j, span])

        def places(k, j, halves):
            span = slice(halves[0] * HALF_PLANE, (halves[-1] + 1) * HALF_PLANE)
            return raw[k, j][:, span].rearrange("p (y dy x dx) -> p dy dx y x", dy=PATCH, x=GRID, dx=PATCH)

        def turn(k, j, half, source, first, last):
            for dx in range(PATCH):
                nc.tensor.matmul(
                    out=by_pixel[k, half][:, j, :],
                    lhsT=source[:, dx, :],
                    rhs=ident_f32[:],
                    is_transpose=True,
                    start=(first and dx == 0),
                    stop=(last and dx == PATCH - 1),
                )

        def add_rows(k, j, dy, halves, pieces):
            width = len(halves) * P
            sums = partial_pool.tile([P, PATCH, width], F32, name="sums_%d" % width)
            for piece in pieces:
                source = places(k, j, piece)
                at = (piece[0] - halves[0]) * P
                nc.vector.tensor_tensor(
                    out=sums[:, :, at : at + len(piece) * P].rearrange("p dx (y x) -> p dx y x", x=GRID),
                    in0=source[:, dy],
                    in1=source[:, dy + ROW_PAIRS],
                    op=ALU.add,
                )
            for position, half in enumerate(halves):
                if j == 0 and dy == 0:
                    by_pixel[k, half] = psum_sums.tile([P, PACK, P], F32, tag="sums", name="by_pixel")
                turn(k, j, half, sums[:, :, position * P : (position + 1) * P], dy == 0, dy == ROW_PAIRS - 1)

        def convert_row(k, j, row):
            converted[k, j, row] = converted_pool.tile([P, PATCH, PIXELS], F32, name="converted")
            nc.scalar.copy(
                out=converted[k, j, row][:].rearrange("p dx (y x) -> p dx y x", x=GRID),
                in_=places(k, j, BOTH)[:, row],
            )

        def turn_converted(k, j, rows):
            for half in BOTH:
                for row in rows:
                    turn(k, j, half, converted[k, j, row][:, :, half * P : (half + 1) * P], False, row == rows[-1])


        def norm_and_scale(k, halves):
            square_sum = small.tile([P, HALVES], F32)
            for half in halves:
                squares = unread.tile([P, CHANNELS], F32)
                nc.scalar.activation(
                    out=squares[:],
                    in_=by_pixel[k, half][:].rearrange("n j p -> n (j p)"),
                    func=ACT.Square,
                    accum_out=square_sum[:, half : half + 1],
                )
            span = slice(halves[0], halves[-1] + 1)
            above_floor = small.tile([P, HALVES], F32)
            nc.scalar.activation(
                out=above_floor[:, span], in_=square_sum[:, span], func=ACT.Relu, bias=-NORM_FLOOR_SQUARED
            )
            inverse = small.tile([P, HALVES], F32)
            nc.scalar.activation(
                out=inverse[:, span], in_=above_floor[:, span], func=ACT.Abs_reciprocal_sqrt, bias=NORM_FLOOR_SQUARED
            )
            for half in halves:
                unit[k, half] = work.tile([P, CHANNELS], BF16, name="unit")
                nc.scalar.activation(
                    out=unit[k, half][:],
                    in_=by_pixel[k, half][:].rearrange("n j p -> n (j p)"),
                    func=ACT.Copy,
                    scale=inverse[:, half : half + 1],
                )

        def turn_back(k, halves):
            back = psum_turn.tile([P, len(halves), PACK, P], BF16, tag="turn", name="back")
            for position, half in enumerate(halves):
                for j in range(PACK):
                    nc.tensor.transpose(
                        back[:, position, j, :], unit[k, half][:, j * P : (j + 1) * P], ident_bf16[:]
                    )
            if halves[0] == 0:
                signs = 2 if is_teacher(k) else 1
                grouped[k] = work.tile([P, signs, PIXELS * PACK], BF16, name="grouped_%d" % signs, align_bytes=64)
            span = slice(halves[0] * P * PACK, (halves[-1] + 1) * P * PACK)
            nc.scalar.copy(
                out=grouped[k][:, 0, span].rearrange("p (h n j) -> p h n j", h=len(halves), j=PACK),
                in_=back[:].rearrange("p h j n -> p h n j"),
            )

        def quantise(k, halves):
            b = k % IMAGES
            if is_teacher(k):
                nc.vector.tensor_scalar_mul(out=grouped[k][:, 1, :], in0=grouped[k][:, 0, :], scalar1=-1.0)
                nc.vector.quantize_mx(
                    out=codes_T[:, b].rearrange("p s n -> p (s n)").bitcast(FP8X4),
                    scales=scales_T[:, b].rearrange("p s n -> p (s n)"),
                    in_=grouped[k][:].rearrange("p s m -> p (s m)"),
                )
            else:
                span = slice(halves[0] * P, (halves[-1] + 1) * P)
                nc.vector.quantize_mx(
                    out=codes_S[:, b, span].bitcast(FP8X4),
                    scales=scales_S[:, b, span],
                    in_=grouped[k][:, 0, span.start * PACK : span.stop * PACK],
                )


        def operand(name, b, span):
            if name == "S":
                return codes_S[:, b, span].bitcast(FP8X4), scales_S[:, b, span]
            sign = 1 if name == "minus_T" else 0
            return codes_T[:, b, sign, span].bitcast(FP8X4), scales_T[:, b, sign, span]

        def similarity(acc, passes, i, half, j):
            for number, (left, right) in enumerate(passes):
                lhs, lhs_scale = operand(left, i, slice(half * P, (half + 1) * P))
                rhs, rhs_scale = operand(right, j, slice(0, PIXELS))
                nc.tensor.matmul_mx(
                    out=acc,
                    lhsT=lhs,
                    lhsT_scale=lhs_scale,
                    rhs=rhs,
                    rhs_scale=rhs_scale,
                    start=(number == 0),
                    stop=(number == len(passes) - 1),
                )

        def shifted_exp(result, sim, row_sum):
            nc.scalar.activation(
                out=result, in_=sim, func=ACT.Exp, scale=INV_TEMPERATURE, bias=-INV_TEMPERATURE, accum_out=row_sum
            )

        def teacher_sims(blocks):
            sim = psum_turn.tile([P, HALVES, PIXELS], F32, tag="turn", name="sim_t")
            for number, (i, half, j) in enumerate(blocks):
                similarity(sim[:, number, :], (("T", "T"),), i, half, j)
            for number, (i, half, j) in enumerate(blocks):
                shifted_exp(exp_t[:, i, j, half, :], sim[:, number, :], z_t[:, i, half, j : j + 1])

        def student_sims(blocks):
            sim = psum_turn.tile([P, HALVES, PIXELS], F32, tag="turn", name="sim_s")
            for number, (i, half, j) in enumerate(blocks):
                similarity(sim[:, number, :], (("S", "S"),), i, half, j)
            for number, (i, half, j) in enumerate(blocks):
                exp_s = unread.tile([P, PIXELS], F32)
                shifted_exp(exp_s[:], sim[:, number, :], z_s[:, i, half, j : j + 1])

        def differences(blocks, pool, tag):
            dif[blocks] = pool.tile([P, HALVES, PIXELS], F32, tag=tag, name="dif")
            for number, (i, half, j) in enumerate(blocks):
                similarity(dif[blocks][:, number, :], (("S", "S"), ("T", "minus_T")), i, half, j)

        def products(blocks):
            for number, (i, half, j) in enumerate(blocks):
                weighted = unread.tile([P, PIXELS], F32)
                nc.vector.scalar_tensor_tensor(
                    out=weighted[:],
                    in0=dif[blocks][:, number, :],
                    scalar=-INV_TEMPERATURE,
                    in1=exp_t[:, i, j, half, :],
                    op0=ALU.mult,
                    op1=ALU.mult,
                    accum_out=cross[:, i, half, j : j + 1],
                )

        def flat(columns):
            return columns[:].rearrange("p i h j -> p (i h j)")


        plan = {}

        def at_step(step, kind, call, *args):
            plan.setdefault((max(0, step), kind), []).append((call, args))

        for k in range(LAST):
            for j in range(PACK):
                step = STEPS * k + ROW_PAIRS * j
                pieces = [(0,), (1,)] if (k, j) == (0, 0) else [BOTH]
                for piece in pieces:
                    at_step(step - ROW_PAIRS * PLANES_AHEAD, LOADS, load, k, j, piece)
                at_step(step, SUMS, add_rows, k, j, 0, BOTH, pieces)
                if (k, j) in CONVERTED:
                    rows = (1, 1 + ROW_PAIRS)
                    for number, row in enumerate(rows):
                        at_step(step - CONVERT_LEAD + 2 * number, CONVERSIONS, convert_row, k, j, row)
                    at_step(step + 1, SUMS, turn_converted, k, j, rows)
                else:
                    at_step(step + 1, SUMS, add_rows, k, j, 1, BOTH, pieces)
        for half in BOTH:
            for j in range(PACK):
                step = STEPS * LAST + PACK * half + j
                at_step(step - ROW_PAIRS * PLANES_AHEAD, LOADS, load, LAST, j, (half,))
                for dy in range(ROW_PAIRS):
                    at_step(step, SUMS, add_rows, LAST, j, dy, (half,), [(half,)])

        for k in range(LAST):
            b = k % IMAGES
            done = STEPS * k + STEPS - 1
            quantised = done + (TEACHER_QUANTISE_DELAY if is_teacher(k) else STUDENT_QUANTISE_DELAY)
            if k == IMAGES:
                quantised += 1
            norm_delay = TEACHER_NORM_DELAY if is_teacher(k) else STUDENT_NORM_DELAY
            at_step(done + norm_delay, STAGES, norm_and_scale, k, BOTH)
            at_step(done + TURN_BACK_DELAY, STAGES, turn_back, k, BOTH)
            at_step(quantised, STAGES, quantise, k, BOTH)
            for number, (i, j) in enumerate(new_pairs(b)):
                blocks = row_blocks(i, j)
                if is_teacher(k):
                    at_step(quantised + 1 + number // TEACHER_PAIRS_A_STEP, PAIRS, teacher_sims, blocks)
                elif k < LAST - 1:
                    at_step(quantised + 1, PAIRS, student_sims, blocks)
                    if b < DEFERRED_FROM:
                        at_step(quantised + 1, PAIRS, differences, blocks, psum_turn, "turn")
                        at_step(quantised + 1 + PRODUCT_DELAY, PRODUCTS, products, blocks)
        done = POOLING_STEPS - PACK - 1
        at_step(done + STUDENT_NORM_DELAY, STAGES, norm_and_scale, LAST, (0,))
        at_step(done + LAST_TURN_BACK_DELAY, STAGES, turn_back, LAST, (0,))
        at_step(done + LAST_QUANTISE_DELAY, STAGES, quantise, LAST, (0,))
        at_step(done + LAST_TURN_BACK_DELAY, STAGES, nc.vector.reciprocal, flat(inv_z), flat(z_t))

        ctx.enter_context(tc.manual_schedule())
        for key in sorted(plan):
            for call, args in plan[key]:
                call(*args)

        b = LAST % IMAGES
        without_last = [row_blocks(i, j) for image in range(DEFERRED_FROM, b) for i, j in new_pairs(image)]
        exps_done = len(new_pairs(DEFERRED_FROM))
        first_half = [(b, 0, j) for j in range(b)]
        second_half = [(b, 0, b)] + [(b, 1, j) for j in range(b + 1)] + [(i, half, b) for i in range(b) for half in BOTH]
        groups = without_last
        for blocks in (first_half, second_half):
            groups = groups + [tuple(blocks[at : at + HALVES]) for at in range(0, len(blocks), HALVES)]

        norm_and_scale(LAST, (1,))
        for number in range(len(groups) + 2):
            if number == LAST_TURN_AT:
                turn_back(LAST, (1,))
            if number == LAST_TURN_AT + 1:
                quantise(LAST, (1,))
            if number >= 2:
                products(groups[number - 2])
            if exps_done < number <= len(groups):
                student_sims(groups[number - 1])
            if number < len(groups):
                differences(groups[number], psum_sums, "sums")

        row_sums = small.tile([P, 3], F32)
        logs = small.tile([P, SOFTMAXES], F32)
        nc.scalar.activation(out=logs[:], in_=flat(inv_z), func=ACT.Ln, accum_out=row_sums[:, 1:2])
        nc.scalar.activation(out=logs[:], in_=flat(z_s), func=ACT.Ln, accum_out=row_sums[:, 2:3])
        expected = small.tile([P, SOFTMAXES], F32)
        nc.vector.scalar_tensor_tensor(
            out=expected[:],
            in0=flat(cross),
            scalar=1.0,
            in1=flat(inv_z),
            op0=ALU.mult,
            op1=ALU.mult,
            accum_out=row_sums[:, 0:1],
        )
        total = psum_turn.tile([P, HALVES, PIXELS], F32, tag="turn", name="total")
        nc.tensor.matmul(out=total[:, 0, 0:3], lhsT=ones[:], rhs=row_sums[:], start=True, stop=True)
        scaled = small.tile([P, 3], F32)
        mean = small.tile([P, 1], F32)
        nc.scalar.activation(
            out=scaled[:],
            in_=total[:, 0, 0:3],
            func=ACT.Copy,
            scale=1.0 / (IMAGES * IMAGES * PIXELS),
            accum_out=mean[:],
        )
        out_view = out
        for axis in range(2 - len(out.shape)):
            out_view = out_view.unsqueeze(0)
        nc.sync.dma_start(out=out_view, in_=mean[0:1, 0:1])
